import numpy as np
import ml_dtypes


def mxq(x, axis, fmt="e4m3"):
    dtype, down = {"e4m3": (ml_dtypes.float8_e4m3fn, 7), "e5m2": (ml_dtypes.float8_e5m2, 14)}[fmt]
    v = np.moveaxis(np.asarray(x, np.float32).astype(ml_dtypes.bfloat16).astype(np.float64), axis, -1)
    blocks = v.reshape(v.shape[:-1] + (-1, 32))
    amax = np.abs(blocks).max(-1, keepdims=True)
    byte = np.maximum(np.where(amax > 0, np.frexp(amax)[1] - 1 + 127, 0) - down, 1)
    scale = np.exp2(byte - 127.0)
    codes = (blocks / scale).astype(np.float32).astype(dtype).astype(np.float64)
    return np.moveaxis((codes * scale).reshape(v.shape), -1, axis)


WIDE = False


def mx_kscale(k):
    if not WIDE:
        return np.ones(k)
    levels = np.array([10, -10, 5, -5, 0])
    a = np.random.permutation(np.resize(levels, k // 512 * 4)).reshape(k // 512, 4)
    idx = np.arange(k)
    return np.exp2(a[idx // 512, idx % 128 // 32])


BF16 = ml_dtypes.bfloat16


def bf(x):
    return np.asarray(x, np.float32).astype(BF16)


def f64(x):
    return np.asarray(x).astype(np.float64)


E2M1 = np.array([0.0, 0.5, 1.0, 1.5, 2.0, 3.0, 4.0, 6.0, -0.0, -0.5, -1.0, -1.5, -2.0, -3.0, -4.0, -6.0])


def pack_weight(w, fmt):
    k, n = w.shape
    w = f64(bf(w)).reshape(k // 32, 32, n)
    amax = np.abs(w).max(1)
    if fmt == "e4m3":
        byte = np.frexp(amax)[1] - 1 + 127 - 7
    else:
        mant, ex = np.frexp(amax / 6.0)
        byte = np.where(mant > 0.5, ex, ex - 1) + 127
    byte = np.clip(np.where(amax > 0, byte, 1), 1, 254)
    scaled = (w * np.exp2(127.0 - byte)[:, None, :]).reshape(k, n).astype(np.float32)
    by_word = np.ascontiguousarray(scaled.reshape(k // 512, 128, 4, n).transpose(0, 1, 3, 2))
    if fmt == "e4m3":
        words = by_word.astype(ml_dtypes.float8_e4m3fn).view(np.uint8)
    else:
        c = by_word.astype(ml_dtypes.float4_e2m1fn).view(np.uint8) & 0xF
        words = c[..., 0::2] | (c[..., 1::2] << 4)
    return np.ascontiguousarray(words), np.ascontiguousarray(byte.astype(np.uint8).reshape(k // 512, 16, n))


def unpack_weight(words, scales, fmt):
    g, p, n, _ = words.shape
    if fmt == "e4m3":
        vals = np.ascontiguousarray(words).view(ml_dtypes.float8_e4m3fn).astype(np.float64)
    else:
        nib = np.empty((g, p, n, 4), np.uint8)
        nib[..., 0::2] = words & 0xF
        nib[..., 1::2] = words >> 4
        vals = E2M1[nib]
    vals = vals * np.repeat(np.exp2(scales.astype(np.float64) - 127.0), 8, axis=1)[..., None]
    return vals.transpose(0, 1, 3, 2).reshape(g * 512, n)


B, S, HID, H, KV, D = 1, 4096, 1024, 2, 1, 128
EPS = 1e-6
THETA = 10000.0
HALF = D // 2
FMT = "e4m3"


def rotate_half(x):
    return np.concatenate([-x[..., HALF:], x[..., :HALF]], axis=-1)


def rms_norm(x, w=None):
    n = x * (1.0 / np.sqrt(np.mean(x * x, axis=-1, keepdims=True) + EPS))
    return n if w is None else n * w


def setup_inputs():
    s = mx_kscale(HID)
    c = 0.004 / np.sqrt(HID)
    inv_freq = 1.0 / THETA ** (np.arange(0, D, 2) / D)
    pos = np.random.randint(0, S) + np.arange(S)
    freqs = pos[:, None] * inv_freq[None, :]
    emb = np.concatenate([freqs, freqs], axis=-1)
    hidden_states = bf(np.random.standard_normal((B, S, HID)) * s)
    Wq_words, Wq_scales = pack_weight((np.random.standard_normal((H * D, HID)) * c / s[None, :]).T, FMT)
    Wk_words, Wk_scales = pack_weight((np.random.standard_normal((KV * D, HID)) * c / s[None, :]).T, FMT)
    Wv_words, Wv_scales = pack_weight((np.random.standard_normal((KV * D, HID)) * c / s[None, :]).T, FMT)
    return {"hidden_states": hidden_states,
            "cos": bf(np.cos(emb)[None]),
            "sin": bf(np.sin(emb)[None]),
            "Wq_words": Wq_words,
            "Wq_scales": Wq_scales,
            "Wk_words": Wk_words,
            "Wk_scales": Wk_scales,
            "Wv_words": Wv_words,
            "Wv_scales": Wv_scales,
            "q_norm_w": bf(0.5 + 0.1 * np.random.standard_normal(D)),
            "k_norm_w": bf(0.5 + 0.1 * np.random.standard_normal(D))}


def reference(hidden_states, cos, sin, Wq_words, Wq_scales, Wk_words, Wk_scales, Wv_words, Wv_scales, q_norm_w, k_norm_w):
    xq = mxq(f64(hidden_states), 2, "e4m3")
    cs = f64(cos)[:, :, None, :]
    sn = f64(sin)[:, :, None, :]
    q = (xq @ unpack_weight(Wq_words, Wq_scales, FMT)).reshape(B, S, H, D)
    k = (xq @ unpack_weight(Wk_words, Wk_scales, FMT)).reshape(B, S, KV, D)
    v = (xq @ unpack_weight(Wv_words, Wv_scales, FMT)).reshape(B, S, KV, D)
    q = rms_norm(q, f64(q_norm_w))
    q = q * cs + rotate_half(q) * sn
    k = rms_norm(k, f64(k_norm_w))
    k = k * cs + rotate_half(k) * sn
    v = rms_norm(v)
    return q.transpose(0, 2, 1, 3), k.transpose(0, 2, 1, 3), v.transpose(0, 2, 1, 3)

@@ -1,0 +1,291 @@
+from contextlib import ExitStack
+
+import concourse.mybir as mybir
+from concourse.masks import make_identity
+
+F32 = mybir.dt.float32
+BF16 = mybir.dt.bfloat16
+I32 = mybir.dt.int32
+U32 = mybir.dt.uint32
+U8 = mybir.dt.uint8
+FP8X4 = mybir.dt.float8_e4m3fn_x4
+ACT = mybir.ActivationFunctionType
+ALU = mybir.AluOpType
+
+P = 128
+PACK = 4
+K_PASS = P * PACK
+TOKENS = 4096
+HID = 1024
+PASSES = HID // K_PASS
+D = 128
+HALF = D // 2
+HEADS = 4
+ROPE_HEADS = 3
+FEATURES = HEADS * D
+TILES = TOKENS // P
+BATCH = 4
+BATCHES = TILES // BATCH
+ROUND = 2
+ROUNDS = TILES // ROUND
+EPS = 1e-6
+
+TRANSPOSE_LEAD = 3
+PROJECT_LEAD = 2
+TABLES_LEAD = 1
+TABLE_BATCHES_AHEAD = 2
+
+FLOPS = 2 * TOKENS * HID * FEATURES
+
+
+def tile_refattention_pa_t_kernel(
+    tc,
+    hidden_states,
+    cos,
+    sin,
+    Wq_words,
+    Wq_scales,
+    Wk_words,
+    Wk_scales,
+    Wv_words,
+    Wv_scales,
+    q_norm_w,
+    k_norm_w,
+    out_0,
+    out_1,
+    out_2,
+):
+    nc = tc.nc
+
+    x_dram = hidden_states.rearrange("b (p t) k -> p (b t) k", t=TILES)
+    cos_dram = cos.rearrange("b (p t) d -> p (b t) d", t=TILES)
+    sin_dram = sin.rearrange("b (p t) d -> p (b t) d", t=TILES)
+    q_dram = out_0.rearrange("b h (p t) d -> p (b h) t d", t=TILES)
+    k_dram = out_1.rearrange("b h (p t) d -> p (b h) t d", t=TILES)
+    v_dram = out_2.rearrange("b h (p t) d -> p (b h) t d", t=TILES)
+
+    def place(n):
+        first_tile = ROUND * n
+        return first_tile // BATCH, first_tile % BATCH
+
+    with ExitStack() as ctx:
+        ctx.enter_context(tc.manual_schedule())
+        keep = ctx.enter_context(tc.tile_pool(name="keep", bufs=1))
+        stage = ctx.enter_context(tc.tile_pool(name="stage", bufs=3))
+        small = ctx.enter_context(tc.tile_pool(name="small", bufs=4 * ROUND))
+        results = ctx.enter_context(tc.tile_pool(name="results", bufs=3))
+        psum_t = ctx.enter_context(tc.psum_pool(name="psum_t", bufs=ROUND))
+        psum_o = ctx.enter_context(tc.psum_pool(name="psum_o", bufs=2 * ROUND))
+        psum_c = ctx.enter_context(tc.psum_pool(name="psum_c", bufs=2))
+
+        x_sb = [keep.tile([P, BATCH, HID], BF16, name="x%d" % b) for b in range(BATCHES)]
+        cos_sb = [keep.tile([P, BATCH, D], BF16, name="cos%d" % b) for b in range(BATCHES)]
+        sin_sb = [keep.tile([P, BATCH, D], BF16, name="sin%d" % b) for b in range(BATCHES)]
+        q_gain = keep.tile([P, D], BF16)
+        k_gain = keep.tile([P, D], BF16)
+        gain_of_head = (q_gain, q_gain, k_gain)
+
+        w_codes = keep.tile([P, PASSES, PACK * FEATURES], U8, align_bytes=64)
+        w_planes = keep.tile([P, PASSES, FEATURES], U8, align_bytes=64)
+        nc.vector.memset(w_planes[:].rearrange("p g n -> p (g n)").bitcast(I32), 0)
+
+        nc.sync.dma_start(out=x_sb[0][:, 0:ROUND, :], in_=x_dram[:, 0:ROUND, :])
+        first_feature = 0
+        for words, scales in ((Wq_words, Wq_scales), (Wk_words, Wk_scales), (Wv_words, Wv_scales)):
+            n_features = words.shape[2]
+            cols = slice(first_feature, first_feature + n_features)
+            byte_cols = slice(PACK * first_feature, PACK * (first_feature + n_features))
+            first_feature += n_features
+            nc.sync.dma_start(
+                out=w_codes[:, :, byte_cols].bitcast(I32),
+                in_=words.rearrange("g p n t -> p g (n t)").bitcast(I32),
+            )
+            for quadrant in range(4):
+                nc.sync.dma_start(
+                    out=w_planes[32 * quadrant : 32 * quadrant + 4, :, cols].bitcast(I32),
+                    in_=scales[:, 4 * quadrant : 4 * quadrant + 4, :]
+                    .rearrange("g q n -> q g n")
+                    .bitcast(I32),
+                )
+        nc.sync.dma_start(out=q_gain[:], in_=q_norm_w.partition_broadcast(P))
+        nc.sync.dma_start(out=k_gain[:], in_=k_norm_w.partition_broadcast(P))
+
+        def load_tables(b):
+            tiles = slice(BATCH * b, BATCH * (b + 1))
+            nc.sync.dma_start(out=cos_sb[b][:], in_=cos_dram[:, tiles, :])
+            nc.sync.dma_start(out=sin_sb[b][:], in_=sin_dram[:, tiles, :])
+
+        for b in range(TABLE_BATCHES_AHEAD):
+            load_tables(b)
+
+        ident = keep.tile([P, P], F32)
+        make_identity(nc, ident[:])
+        nc.gpsimd.dma_start(out=x_sb[0][:, ROUND:BATCH, :], in_=x_dram[:, ROUND:BATCH, :])
+        for b in range(1, BATCHES):
+            nc.gpsimd.dma_start(out=x_sb[b][:], in_=x_dram[:, BATCH * b : BATCH * (b + 1), :])
+        plus_one = keep.tile([P, P], BF16)
+        nc.vector.tensor_copy(out=plus_one[:], in_=ident[:])
+        minus_one = keep.tile([P, P], BF16)
+        nc.vector.tensor_scalar_mul(out=minus_one[:], in0=ident[:], scalar1=-1.0)
+        eps = keep.tile([P, 1], F32)
+        nc.vector.memset(eps[:], EPS)
+
+        low = slice(0, HALF)
+        high = slice(HALF, D)
+
+        grouped = {}
+        codes = {}
+        planes = {}
+        products = {}
+        rstd = {}
+        normed = {}
+        tables = {}
+        rotated = {}
+        value = {}
+
+        def transpose_round(n):
+            b, first = place(n)
+            grouped[n] = stage.tile([P, ROUND, PASSES, P, PACK], BF16, align_bytes=64, name="grouped")
+            for j in range(ROUND):
+                words = x_sb[b][:, first + j, :].bitcast(F32)
+                xt = psum_t.tile([P, PASSES, 2, P], F32)
+                for g in range(PASSES):
+                    for u in range(2):
+                        nc.tensor.transpose(
+                            xt[:, g, u, :],
+                            words[:, 2 * P * g + u : 2 * P * (g + 1) : 2],
+                            ident[:],
+                        )
+                nc.scalar.copy(
+                    out=grouped[n][:, j]
+                    .rearrange("p g r t -> p (g r t)")
+                    .bitcast(F32)
+                    .rearrange("p (g r u) -> p g r u", g=PASSES, u=2),
+                    in_=xt[:].rearrange("p g u r -> p g r u"),
+                )
+
+        def quantise_round(n):
+            codes[n] = stage.tile([P, ROUND, PASSES, P], U32, align_bytes=64, name="codes")
+            planes[n] = stage.tile([P, ROUND, PASSES, P], U8, align_bytes=64, name="planes")
+            for j in range(ROUND):
+                nc.vector.quantize_mx(
+                    out=codes[n][:, j].rearrange("p g r -> p (g r)").bitcast(FP8X4),
+                    scales=planes[n][:, j].rearrange("p g r -> p (g r)"),
+                    in_=grouped[n][:, j].rearrange("p g r t -> p (g r t)"),
+                )
+
+        def project_round(n):
+            for j in range(ROUND):
+                acc = psum_o.tile([P, FEATURES], F32)
+                for g in range(PASSES):
+                    nc.tensor.matmul_mx(
+                        out=acc[:],
+                        lhsT=codes[n][:, j, g, :].bitcast(FP8X4),
+                        lhsT_scale=planes[n][:, j, g, :],
+                        rhs=w_codes[:, g, :].bitcast(FP8X4),
+                        rhs_scale=w_planes[:, g, :],
+                        start=(g == 0),
+                        stop=(g == PASSES - 1),
+                    )
+                square_sum = small.tile([P, HEADS], F32)
+                for h in range(HEADS):
+                    squares = stage.tile([P, D], BF16)
+                    nc.scalar.activation(
+                        out=squares[:],
+                        in_=acc[:, D * h : D * (h + 1)],
+                        func=ACT.Square,
+                        accum_out=square_sum[:, h : h + 1],
+                    )
+                inv_rms = small.tile([P, HEADS], F32)
+                nc.scalar.activation(
+                    out=inv_rms[:],
+                    in_=square_sum[:],
+                    func=ACT.Abs_reciprocal_sqrt,
+                    bias=eps[:],
+                    scale=1.0 / D,
+                )
+                products[n, j] = acc
+                rstd[n, j] = inv_rms
+
+        def tables_round(n):
+            b, first = place(n)
+            tiles = slice(first, first + ROUND)
+            tables[n] = psum_c.tile([P, 2, ROUND, D], F32, name="tables")
+            nc.tensor.matmul(
+                out=tables[n][:, 0], lhsT=plus_one[:], rhs=cos_sb[b][:, tiles, :], start=True, stop=True
+            )
+            nc.tensor.matmul(
+                out=tables[n][:, 1, :, low], lhsT=minus_one[:], rhs=sin_sb[b][:, tiles, low], start=True, stop=True
+            )
+            nc.tensor.matmul(
+                out=tables[n][:, 1, :, high], lhsT=plus_one[:], rhs=sin_sb[b][:, tiles, high], start=True, stop=True
+            )
+
+        def normalise_round(n):
+            b, first = place(n)
+            normed[n] = stage.tile([P, ROPE_HEADS, ROUND, D], F32, name="normed")
+            if first == 0:
+                value[b] = results.tile([P, BATCH, D], F32, name="value")
+            for j in range(ROUND):
+                acc = products[n, j]
+                for h in range(ROPE_HEADS):
+                    nc.vector.scalar_tensor_tensor(
+                        out=normed[n][:, h, j, :],
+                        in0=acc[:, D * h : D * (h + 1)],
+                        scalar=rstd[n, j][:, h : h + 1],
+                        in1=gain_of_head[h][:],
+                        op0=ALU.mult,
+                        op1=ALU.mult,
+                    )
+                nc.scalar.activation(
+                    out=value[b][:, first + j, :],
+                    in_=acc[:, D * ROPE_HEADS : FEATURES],
+                    func=ACT.Copy,
+                    scale=rstd[n, j][:, ROPE_HEADS : HEADS],
+                )
+
+        def rotate_round(n):
+            b, first = place(n)
+            u = normed[n]
+            shape = [P, ROPE_HEADS, ROUND, D]
+            cos_heads = tables[n][:, 0].unsqueeze(1).to_broadcast(shape)
+            sin_heads = tables[n][:, 1].unsqueeze(1).to_broadcast(shape)
+            straight = stage.tile(shape, F32)
+            crossed = stage.tile(shape, F32)
+            if first == 0:
+                rotated[b] = results.tile([P, ROPE_HEADS, BATCH, D], F32, name="rotated")
+            nc.vector.tensor_tensor(out=straight[:], in0=u[:], in1=cos_heads, op=ALU.mult)
+            nc.vector.tensor_tensor(
+                out=crossed[:, :, :, low], in0=u[:, :, :, high], in1=sin_heads[:, :, :, low], op=ALU.mult
+            )
+            nc.vector.tensor_tensor(
+                out=crossed[:, :, :, high], in0=u[:, :, :, low], in1=sin_heads[:, :, :, high], op=ALU.mult
+            )
+            for h in range(ROPE_HEADS):
+                nc.gpsimd.tensor_tensor(
+                    out=rotated[b][:, h, first : first + ROUND, :],
+                    in0=straight[:, h],
+                    in1=crossed[:, h],
+                    op=ALU.add,
+                )
+            if first + ROUND == BATCH:
+                tiles = slice(BATCH * b, BATCH * (b + 1))
+                nc.sync.dma_start(out=v_dram[:, 0, tiles, :], in_=value[b][:])
+                nc.sync.dma_start(out=q_dram[:, :, tiles, :], in_=rotated[b][:, 0:2, :, :])
+                nc.sync.dma_start(out=k_dram[:, 0, tiles, :], in_=rotated[b][:, 2, :, :])
+
+        for n in range(-TRANSPOSE_LEAD, ROUNDS):
+            if 0 <= n + TABLES_LEAD < ROUNDS:
+                tables_round(n + TABLES_LEAD)
+            if n >= 0:
+                b, first = place(n)
+                if first == 0 and b + TABLE_BATCHES_AHEAD < BATCHES:
+                    load_tables(b + TABLE_BATCHES_AHEAD)
+                normalise_round(n)
+            if n + TRANSPOSE_LEAD < ROUNDS:
+                transpose_round(n + TRANSPOSE_LEAD)
+            if 0 <= n + PROJECT_LEAD < ROUNDS:
+                quantise_round(n + PROJECT_LEAD)
+                project_round(n + PROJECT_LEAD)
+            if n >= 0:
+                rotate_round(n)

@@ -30,8 +30,10 @@ ROUND = 2
 ROUNDS = TILES // ROUND
 EPS = 1e-6
 
-TRANSPOSE_LEAD = 3
+TRANSPOSE_LEAD = 4
+QUANTISE_LEAD = 3
 PROJECT_LEAD = 2
+NORMALISE_LEAD = 1
 TABLES_LEAD = 1
 TABLE_BATCHES_AHEAD = 2
 
@@ -167,12 +169,11 @@ def tile_refattention_pa_t_kernel(
         def quantise_round(n):
             codes[n] = stage.tile([P, ROUND, PASSES, P], U32, align_bytes=64, name="codes")
             planes[n] = stage.tile([P, ROUND, PASSES, P], U8, align_bytes=64, name="planes")
-            for j in range(ROUND):
-                nc.vector.quantize_mx(
-                    out=codes[n][:, j].rearrange("p g r -> p (g r)").bitcast(FP8X4),
-                    scales=planes[n][:, j].rearrange("p g r -> p (g r)"),
-                    in_=grouped[n][:, j].rearrange("p g r t -> p (g r t)"),
-                )
+            nc.vector.quantize_mx(
+                out=codes[n][:].rearrange("p j g r -> p (j g r)").bitcast(FP8X4),
+                scales=planes[n][:].rearrange("p j g r -> p (j g r)"),
+                in_=grouped[n][:].rearrange("p j g r t -> p (j g r t)"),
+            )
 
         def project_round(n):
             for j in range(ROUND):
@@ -275,17 +276,19 @@ def tile_refattention_pa_t_kernel(
                 nc.sync.dma_start(out=k_dram[:, 0, tiles, :], in_=rotated[b][:, 2, :, :])
 
         for n in range(-TRANSPOSE_LEAD, ROUNDS):
-            if 0 <= n + TABLES_LEAD < ROUNDS:
-                tables_round(n + TABLES_LEAD)
             if n >= 0:
                 b, first = place(n)
                 if first == 0 and b + TABLE_BATCHES_AHEAD < BATCHES:
                     load_tables(b + TABLE_BATCHES_AHEAD)
-                normalise_round(n)
+            if 0 <= n + NORMALISE_LEAD < ROUNDS:
+                normalise_round(n + NORMALISE_LEAD)
+            if 0 <= n + PROJECT_LEAD < ROUNDS:
+                project_round(n + PROJECT_LEAD)
+            if 0 <= n + TABLES_LEAD < ROUNDS:
+                tables_round(n + TABLES_LEAD)
             if n + TRANSPOSE_LEAD < ROUNDS:
                 transpose_round(n + TRANSPOSE_LEAD)
-            if 0 <= n + PROJECT_LEAD < ROUNDS:
-                quantise_round(n + PROJECT_LEAD)
-                project_round(n + PROJECT_LEAD)
             if n >= 0:
                 rotate_round(n)
+            if 0 <= n + QUANTISE_LEAD < ROUNDS:
+                quantise_round(n + QUANTISE_LEAD)

@@ -127,8 +127,6 @@ def tile_refattention_pa_t_kernel(
             nc.gpsimd.dma_start(out=x_sb[b][:], in_=x_dram[:, BATCH * b : BATCH * (b + 1), :])
         plus_one = keep.tile([P, P], BF16)
         nc.vector.tensor_copy(out=plus_one[:], in_=ident[:])
-        minus_one = keep.tile([P, P], BF16)
-        nc.vector.tensor_scalar_mul(out=minus_one[:], in0=ident[:], scalar1=-1.0)
         eps = keep.tile([P, 1], F32)
         nc.vector.memset(eps[:], EPS)
 
@@ -216,10 +214,10 @@ def tile_refattention_pa_t_kernel(
                 out=tables[n][:, 0], lhsT=plus_one[:], rhs=cos_sb[b][:, tiles, :], start=True, stop=True
             )
             nc.tensor.matmul(
-                out=tables[n][:, 1, :, low], lhsT=minus_one[:], rhs=sin_sb[b][:, tiles, low], start=True, stop=True
+                out=tables[n][:, 1, :, low], lhsT=plus_one[:], rhs=sin_sb[b][:, tiles, high], start=True, stop=True
             )
             nc.tensor.matmul(
-                out=tables[n][:, 1, :, high], lhsT=plus_one[:], rhs=sin_sb[b][:, tiles, high], start=True, stop=True
+                out=tables[n][:, 1, :, high], lhsT=plus_one[:], rhs=sin_sb[b][:, tiles, low], start=True, stop=True
             )
 
         def normalise_round(n):
@@ -245,35 +243,36 @@ def tile_refattention_pa_t_kernel(
                     scale=rstd[n, j][:, ROPE_HEADS : HEADS],
                 )
 
+        def store(b, start, stop):
+            tiles = slice(BATCH * b + start, BATCH * b + stop)
+            nc.sync.dma_start(out=v_dram[:, 0, tiles, :], in_=value[b][:, start:stop, :])
+            nc.sync.dma_start(out=q_dram[:, :, tiles, :], in_=rotated[b][:, 0:2, start:stop, :])
+            nc.sync.dma_start(out=k_dram[:, 0, tiles, :], in_=rotated[b][:, 2, start:stop, :])
+
         def rotate_round(n):
             b, first = place(n)
-            u = normed[n]
-            shape = [P, ROPE_HEADS, ROUND, D]
-            cos_heads = tables[n][:, 0].unsqueeze(1).to_broadcast(shape)
-            sin_heads = tables[n][:, 1].unsqueeze(1).to_broadcast(shape)
-            straight = stage.tile(shape, F32)
-            crossed = stage.tile(shape, F32)
+            shape = [P, 2, ROPE_HEADS, ROUND * D]
+            both = stage.tile([P, 2, ROPE_HEADS, ROUND, D], F32)
             if first == 0:
                 rotated[b] = results.tile([P, ROPE_HEADS, BATCH, D], F32, name="rotated")
-            nc.vector.tensor_tensor(out=straight[:], in0=u[:], in1=cos_heads, op=ALU.mult)
             nc.vector.tensor_tensor(
-                out=crossed[:, :, :, low], in0=u[:, :, :, high], in1=sin_heads[:, :, :, low], op=ALU.mult
+                out=both[:].rearrange("p w h j d -> p w h (j d)"),
+                in0=normed[n][:].rearrange("p h j d -> p h (j d)").unsqueeze(1).to_broadcast(shape),
+                in1=tables[n][:].rearrange("p w j d -> p w (j d)").unsqueeze(2).to_broadcast(shape),
+                op=ALU.mult,
             )
-            nc.vector.tensor_tensor(
-                out=crossed[:, :, :, high], in0=u[:, :, :, low], in1=sin_heads[:, :, :, high], op=ALU.mult
+            tiles = slice(first, first + ROUND)
+            joiner = nc.vector if n == ROUNDS - 1 else nc.gpsimd
+            joiner.tensor_tensor(
+                out=rotated[b][:, :, tiles, low], in0=both[:, 0, :, :, low], in1=both[:, 1, :, :, high], op=ALU.subtract
             )
-            for h in range(ROPE_HEADS):
-                nc.gpsimd.tensor_tensor(
-                    out=rotated[b][:, h, first : first + ROUND, :],
-                    in0=straight[:, h],
-                    in1=crossed[:, h],
-                    op=ALU.add,
-                )
-            if first + ROUND == BATCH:
-                tiles = slice(BATCH * b, BATCH * (b + 1))
-                nc.sync.dma_start(out=v_dram[:, 0, tiles, :], in_=value[b][:])
-                nc.sync.dma_start(out=q_dram[:, :, tiles, :], in_=rotated[b][:, 0:2, :, :])
-                nc.sync.dma_start(out=k_dram[:, 0, tiles, :], in_=rotated[b][:, 2, :, :])
+            joiner.tensor_tensor(
+                out=rotated[b][:, :, tiles, high], in0=both[:, 0, :, :, high], in1=both[:, 1, :, :, low], op=ALU.add
+            )
+            if b == BATCHES - 1:
+                store(b, first, first + ROUND)
+            elif first + ROUND == BATCH:
+                store(b, 0, BATCH)
 
         for n in range(-TRANSPOSE_LEAD, ROUNDS):
             if n >= 0:

@@ -22,6 +22,7 @@ D = 128
 HALF = D // 2
 HEADS = 4
 ROPE_HEADS = 3
+QUERY_HEADS = 2
 FEATURES = HEADS * D
 TILES = TOKENS // P
 BATCH = 4
@@ -140,6 +141,7 @@ def tile_refattention_pa_t_kernel(
         rstd = {}
         normed = {}
         tables = {}
+        products_of = {}
         rotated = {}
         value = {}
 
@@ -243,6 +245,17 @@ def tile_refattention_pa_t_kernel(
                     scale=rstd[n, j][:, ROPE_HEADS : HEADS],
                 )
 
+        def key_times_cos_round(n):
+            b, first = place(n)
+            both = stage.tile([P, 2, ROPE_HEADS, ROUND, D], F32, name="both")
+            products_of[n] = both
+            nc.gpsimd.tensor_tensor(
+                out=both[:, 0, QUERY_HEADS],
+                in0=normed[n][:, QUERY_HEADS],
+                in1=cos_sb[b][:, first : first + ROUND, :],
+                op=ALU.mult,
+            )
+
         def store(b, start, stop):
             tiles = slice(BATCH * b + start, BATCH * b + stop)
             nc.sync.dma_start(out=v_dram[:, 0, tiles, :], in_=value[b][:, start:stop, :])
@@ -251,14 +264,21 @@ def tile_refattention_pa_t_kernel(
 
         def rotate_round(n):
             b, first = place(n)
-            shape = [P, 2, ROPE_HEADS, ROUND * D]
-            both = stage.tile([P, 2, ROPE_HEADS, ROUND, D], F32)
+            both = products_of[n]
             if first == 0:
                 rotated[b] = results.tile([P, ROPE_HEADS, BATCH, D], F32, name="rotated")
+            u = normed[n][:].rearrange("p h j d -> p h (j d)")
+            table = tables[n][:].rearrange("p w j d -> p w (j d)")
             nc.vector.tensor_tensor(
-                out=both[:].rearrange("p w h j d -> p w h (j d)"),
-                in0=normed[n][:].rearrange("p h j d -> p h (j d)").unsqueeze(1).to_broadcast(shape),
-                in1=tables[n][:].rearrange("p w j d -> p w (j d)").unsqueeze(2).to_broadcast(shape),
+                out=both[:, 0, 0:QUERY_HEADS].rearrange("p h j d -> p h (j d)"),
+                in0=u[:, 0:QUERY_HEADS],
+                in1=table[:, 0].unsqueeze(1).to_broadcast([P, QUERY_HEADS, ROUND * D]),
+                op=ALU.mult,
+            )
+            nc.vector.tensor_tensor(
+                out=both[:, 1].rearrange("p h j d -> p h (j d)"),
+                in0=u,
+                in1=table[:, 1].unsqueeze(1).to_broadcast([P, ROPE_HEADS, ROUND * D]),
                 op=ALU.mult,
             )
             tiles = slice(first, first + ROUND)
@@ -281,6 +301,7 @@ def tile_refattention_pa_t_kernel(
                     load_tables(b + TABLE_BATCHES_AHEAD)
             if 0 <= n + NORMALISE_LEAD < ROUNDS:
                 normalise_round(n + NORMALISE_LEAD)
+                key_times_cos_round(n + NORMALISE_LEAD)
             if 0 <= n + PROJECT_LEAD < ROUNDS:
                 project_round(n + PROJECT_LEAD)
             if 0 <= n + TABLES_LEAD < ROUNDS:

@@ -238,11 +238,10 @@ def tile_refattention_pa_t_kernel(
                         op0=ALU.mult,
                         op1=ALU.mult,
                     )
-                nc.scalar.activation(
+                nc.vector.tensor_scalar_mul(
                     out=value[b][:, first + j, :],
-                    in_=acc[:, D * ROPE_HEADS : FEATURES],
-                    func=ACT.Copy,
-                    scale=rstd[n, j][:, ROPE_HEADS : HEADS],
+                    in0=acc[:, D * ROPE_HEADS : FEATURES],
+                    scalar1=rstd[n, j][:, ROPE_HEADS : HEADS],
                 )
 
         def key_times_cos_round(n):

@@ -31,11 +31,13 @@ ROUND = 2
 ROUNDS = TILES // ROUND
 EPS = 1e-6
 
-TRANSPOSE_LEAD = 4
-QUANTISE_LEAD = 3
+TRANSPOSE_LEAD = 5
+QUANTISE_LEAD = 4
 PROJECT_LEAD = 2
 NORMALISE_LEAD = 1
 TABLES_LEAD = 1
+SHARED_ROUNDS = 3
+X_BATCHES_AHEAD = 4
 TABLE_BATCHES_AHEAD = 2
 
 FLOPS = 2 * TOKENS * HID * FEATURES
@@ -74,7 +76,7 @@ def tile_refattention_pa_t_kernel(
     with ExitStack() as ctx:
         ctx.enter_context(tc.manual_schedule())
         keep = ctx.enter_context(tc.tile_pool(name="keep", bufs=1))
-        stage = ctx.enter_context(tc.tile_pool(name="stage", bufs=3))
+        stage = ctx.enter_context(tc.tile_pool(name="stage", bufs=4))
         small = ctx.enter_context(tc.tile_pool(name="small", bufs=4 * ROUND))
         results = ctx.enter_context(tc.tile_pool(name="results", bufs=3))
         psum_t = ctx.enter_context(tc.psum_pool(name="psum_t", bufs=ROUND))
@@ -92,17 +94,29 @@ def tile_refattention_pa_t_kernel(
         w_planes = keep.tile([P, PASSES, FEATURES], U8, align_bytes=64)
         nc.vector.memset(w_planes[:].rearrange("p g n -> p (g n)").bitcast(I32), 0)
 
-        nc.sync.dma_start(out=x_sb[0][:, 0:ROUND, :], in_=x_dram[:, 0:ROUND, :])
-        first_feature = 0
-        for words, scales in ((Wq_words, Wq_scales), (Wk_words, Wk_scales), (Wv_words, Wv_scales)):
+        def load_x(b, start=0, stop=BATCH):
+            nc.sync.dma_start(
+                out=x_sb[b][:, start:stop, :], in_=x_dram[:, BATCH * b + start : BATCH * b + stop, :]
+            )
+
+        def load_tables(b):
+            tiles = slice(BATCH * b, BATCH * (b + 1))
+            nc.sync.dma_start(out=cos_sb[b][:], in_=cos_dram[:, tiles, :])
+            nc.sync.dma_start(out=sin_sb[b][:], in_=sin_dram[:, tiles, :])
+
+        for t in range(ROUND):
+            load_x(0, t, t + 1)
+        weights = ((Wq_words, Wq_scales, 0), (Wk_words, Wk_scales, QUERY_HEADS * D), (Wv_words, Wv_scales, ROPE_HEADS * D))
+        for words, scales, first_feature in weights:
             n_features = words.shape[2]
-            cols = slice(first_feature, first_feature + n_features)
             byte_cols = slice(PACK * first_feature, PACK * (first_feature + n_features))
-            first_feature += n_features
             nc.sync.dma_start(
                 out=w_codes[:, :, byte_cols].bitcast(I32),
                 in_=words.rearrange("g p n t -> p g (n t)").bitcast(I32),
             )
+        load_x(0, ROUND, BATCH)
+        for words, scales, first_feature in weights:
+            cols = slice(first_feature, first_feature + words.shape[2])
             for quadrant in range(4):
                 nc.sync.dma_start(
                     out=w_planes[32 * quadrant : 32 * quadrant + 4, :, cols].bitcast(I32),
@@ -110,26 +124,23 @@ def tile_refattention_pa_t_kernel(
                     .rearrange("g q n -> q g n")
                     .bitcast(I32),
                 )
+        load_tables(0)
         nc.sync.dma_start(out=q_gain[:], in_=q_norm_w.partition_broadcast(P))
         nc.sync.dma_start(out=k_gain[:], in_=k_norm_w.partition_broadcast(P))
+        load_x(1, 0, ROUND)
+        load_x(1, ROUND, BATCH)
+        load_x(2)
+        load_tables(1)
+        load_x(3)
 
-        def load_tables(b):
-            tiles = slice(BATCH * b, BATCH * (b + 1))
-            nc.sync.dma_start(out=cos_sb[b][:], in_=cos_dram[:, tiles, :])
-            nc.sync.dma_start(out=sin_sb[b][:], in_=sin_dram[:, tiles, :])
-
-        for b in range(TABLE_BATCHES_AHEAD):
-            load_tables(b)
-
-        ident = keep.tile([P, P], F32)
-        make_identity(nc, ident[:])
-        nc.gpsimd.dma_start(out=x_sb[0][:, ROUND:BATCH, :], in_=x_dram[:, ROUND:BATCH, :])
-        for b in range(1, BATCHES):
-            nc.gpsimd.dma_start(out=x_sb[b][:], in_=x_dram[:, BATCH * b : BATCH * (b + 1), :])
-        plus_one = keep.tile([P, P], BF16)
-        nc.vector.tensor_copy(out=plus_one[:], in_=ident[:])
         eps = keep.tile([P, 1], F32)
         nc.vector.memset(eps[:], EPS)
+        warm = keep.tile([P, 1], F32)
+        nc.scalar.activation(out=warm[:], in_=eps[:], func=ACT.Abs_reciprocal_sqrt)
+        ident = keep.tile([P, P], F32)
+        make_identity(nc, ident[:])
+        plus_one = keep.tile([P, P], BF16)
+        nc.vector.tensor_copy(out=plus_one[:], in_=ident[:])
 
         low = slice(0, HALF)
         high = slice(HALF, D)
@@ -138,6 +149,7 @@ def tile_refattention_pa_t_kernel(
         codes = {}
         planes = {}
         products = {}
+        square_sums = {}
         rstd = {}
         normed = {}
         tables = {}
@@ -158,7 +170,8 @@ def tile_refattention_pa_t_kernel(
                             words[:, 2 * P * g + u : 2 * P * (g + 1) : 2],
                             ident[:],
                         )
-                nc.scalar.copy(
+                copy_out = nc.vector.tensor_copy if n < SHARED_ROUNDS and j == 1 else nc.scalar.copy
+                copy_out(
                     out=grouped[n][:, j]
                     .rearrange("p g r t -> p (g r t)")
                     .bitcast(F32)
@@ -176,6 +189,7 @@ def tile_refattention_pa_t_kernel(
             )
 
         def project_round(n):
+            square_sums[n] = small.tile([P, ROUND, HEADS], F32, name="square_sum")
             for j in range(ROUND):
                 acc = psum_o.tile([P, FEATURES], F32)
                 for g in range(PASSES):
@@ -188,25 +202,27 @@ def tile_refattention_pa_t_kernel(
                         start=(g == 0),
                         stop=(g == PASSES - 1),
                     )
-                square_sum = small.tile([P, HEADS], F32)
                 for h in range(HEADS):
                     squares = stage.tile([P, D], BF16)
                     nc.scalar.activation(
                         out=squares[:],
                         in_=acc[:, D * h : D * (h + 1)],
                         func=ACT.Square,
-                        accum_out=square_sum[:, h : h + 1],
+                        accum_out=square_sums[n][:, j, h : h + 1],
                     )
-                inv_rms = small.tile([P, HEADS], F32)
-                nc.scalar.activation(
-                    out=inv_rms[:],
-                    in_=square_sum[:],
-                    func=ACT.Abs_reciprocal_sqrt,
-                    bias=eps[:],
-                    scale=1.0 / D,
-                )
                 products[n, j] = acc
-                rstd[n, j] = inv_rms
+
+        def inverse_rms_round(n):
+            inv_rms = small.tile([P, ROUND, HEADS], F32)
+            nc.scalar.activation(
+                out=inv_rms[:].rearrange("p j h -> p (j h)"),
+                in_=square_sums[n][:].rearrange("p j h -> p (j h)"),
+                func=ACT.Abs_reciprocal_sqrt,
+                bias=eps[:],
+                scale=1.0 / D,
+            )
+            for j in range(ROUND):
+                rstd[n, j] = inv_rms[:, j, :]
 
         def tables_round(n):
             b, first = place(n)
@@ -293,21 +309,42 @@ def tile_refattention_pa_t_kernel(
             elif first + ROUND == BATCH:
                 store(b, 0, BATCH)
 
-        for n in range(-TRANSPOSE_LEAD, ROUNDS):
-            if n >= 0:
-                b, first = place(n)
-                if first == 0 and b + TABLE_BATCHES_AHEAD < BATCHES:
-                    load_tables(b + TABLE_BATCHES_AHEAD)
-            if 0 <= n + NORMALISE_LEAD < ROUNDS:
-                normalise_round(n + NORMALISE_LEAD)
-                key_times_cos_round(n + NORMALISE_LEAD)
-            if 0 <= n + PROJECT_LEAD < ROUNDS:
+        def start_normalise(n):
+            normalise_round(n)
+            key_times_cos_round(n)
+
+        transpose_round(0)
+        quantise_round(0)
+        transpose_round(1)
+        project_round(0)
+        inverse_rms_round(0)
+        quantise_round(1)
+        tables_round(0)
+        start_normalise(0)
+        transpose_round(2)
+        project_round(1)
+        inverse_rms_round(1)
+        quantise_round(2)
+        next_transpose = 3
+        next_quantise = 3
+        for n in range(ROUNDS):
+            b, first = place(n)
+            if first == 0 and b + X_BATCHES_AHEAD < BATCHES:
+                load_x(b + X_BATCHES_AHEAD)
+            if first == 0 and b + TABLE_BATCHES_AHEAD < BATCHES:
+                load_tables(b + TABLE_BATCHES_AHEAD)
+            if n + NORMALISE_LEAD < ROUNDS:
+                start_normalise(n + NORMALISE_LEAD)
+            if n + PROJECT_LEAD < ROUNDS:
                 project_round(n + PROJECT_LEAD)
-            if 0 <= n + TABLES_LEAD < ROUNDS:
+            if n + TABLES_LEAD < ROUNDS:
                 tables_round(n + TABLES_LEAD)
-            if n + TRANSPOSE_LEAD < ROUNDS:
-                transpose_round(n + TRANSPOSE_LEAD)
-            if n >= 0:
-                rotate_round(n)
-            if 0 <= n + QUANTISE_LEAD < ROUNDS:
-                quantise_round(n + QUANTISE_LEAD)
+            while next_transpose <= min(n + TRANSPOSE_LEAD, 2 * n + 4, ROUNDS - 1):
+                transpose_round(next_transpose)
+                next_transpose += 1
+            if n + PROJECT_LEAD < ROUNDS:
+                inverse_rms_round(n + PROJECT_LEAD)
+            rotate_round(n)
+            while next_quantise <= min(n + QUANTISE_LEAD, 2 * n + 3, ROUNDS - 1):
+                quantise_round(next_quantise)
+                next_quantise += 1

@@ -78,12 +78,13 @@ def tile_refattention_pa_t_kernel(
         keep = ctx.enter_context(tc.tile_pool(name="keep", bufs=1))
         stage = ctx.enter_context(tc.tile_pool(name="stage", bufs=4))
         small = ctx.enter_context(tc.tile_pool(name="small", bufs=4 * ROUND))
+        inputs = ctx.enter_context(tc.tile_pool(name="inputs", bufs=5))
         results = ctx.enter_context(tc.tile_pool(name="results", bufs=3))
         psum_t = ctx.enter_context(tc.psum_pool(name="psum_t", bufs=ROUND))
         psum_o = ctx.enter_context(tc.psum_pool(name="psum_o", bufs=2 * ROUND))
         psum_c = ctx.enter_context(tc.psum_pool(name="psum_c", bufs=2))
 
-        x_sb = [keep.tile([P, BATCH, HID], BF16, name="x%d" % b) for b in range(BATCHES)]
+        x_sb = {}
         cos_sb = [keep.tile([P, BATCH, D], BF16, name="cos%d" % b) for b in range(BATCHES)]
         sin_sb = [keep.tile([P, BATCH, D], BF16, name="sin%d" % b) for b in range(BATCHES)]
         q_gain = keep.tile([P, D], BF16)
@@ -95,6 +96,8 @@ def tile_refattention_pa_t_kernel(
         nc.vector.memset(w_planes[:].rearrange("p g n -> p (g n)").bitcast(I32), 0)
 
         def load_x(b, start=0, stop=BATCH):
+            if start == 0:
+                x_sb[b] = inputs.tile([P, BATCH, HID], BF16, name="x")
             nc.sync.dma_start(
                 out=x_sb[b][:, start:stop, :], in_=x_dram[:, BATCH * b + start : BATCH * b + stop, :]
             )
@@ -141,6 +144,8 @@ def tile_refattention_pa_t_kernel(
         make_identity(nc, ident[:])
         plus_one = keep.tile([P, P], BF16)
         nc.vector.tensor_copy(out=plus_one[:], in_=ident[:])
+        minus_one = keep.tile([P, P], BF16)
+        nc.vector.tensor_scalar_mul(out=minus_one[:], in0=ident[:], scalar1=-1.0)
 
         low = slice(0, HALF)
         high = slice(HALF, D)
@@ -180,8 +185,8 @@ def tile_refattention_pa_t_kernel(
                 )
 
         def quantise_round(n):
-            codes[n] = stage.tile([P, ROUND, PASSES, P], U32, align_bytes=64, name="codes")
-            planes[n] = stage.tile([P, ROUND, PASSES, P], U8, align_bytes=64, name="planes")
+            codes[n] = keep.tile([P, ROUND, PASSES, P], U32, align_bytes=64, name="codes%d" % n)
+            planes[n] = keep.tile([P, ROUND, PASSES, P], U8, align_bytes=64, name="planes%d" % n)
             nc.vector.quantize_mx(
                 out=codes[n][:].rearrange("p j g r -> p (j g r)").bitcast(FP8X4),
                 scales=planes[n][:].rearrange("p j g r -> p (j g r)"),
@@ -232,17 +237,17 @@ def tile_refattention_pa_t_kernel(
                 out=tables[n][:, 0], lhsT=plus_one[:], rhs=cos_sb[b][:, tiles, :], start=True, stop=True
             )
             nc.tensor.matmul(
-                out=tables[n][:, 1, :, low], lhsT=plus_one[:], rhs=sin_sb[b][:, tiles, high], start=True, stop=True
+                out=tables[n][:, 1, :, low], lhsT=minus_one[:], rhs=sin_sb[b][:, tiles, low], start=True, stop=True
             )
             nc.tensor.matmul(
-                out=tables[n][:, 1, :, high], lhsT=plus_one[:], rhs=sin_sb[b][:, tiles, low], start=True, stop=True
+                out=tables[n][:, 1, :, high], lhsT=plus_one[:], rhs=sin_sb[b][:, tiles, high], start=True, stop=True
             )
 
         def normalise_round(n):
             b, first = place(n)
-            normed[n] = stage.tile([P, ROPE_HEADS, ROUND, D], F32, name="normed")
+            normed[n] = keep.tile([P, ROPE_HEADS, ROUND, D], F32, name="normed%d" % n)
             if first == 0:
-                value[b] = results.tile([P, BATCH, D], F32, name="value")
+                value[b] = keep.tile([P, BATCH, D], F32, name="value%d" % b)
             for j in range(ROUND):
                 acc = products[n, j]
                 for h in range(ROPE_HEADS):
@@ -291,18 +296,18 @@ def tile_refattention_pa_t_kernel(
                 op=ALU.mult,
             )
             nc.vector.tensor_tensor(
-                out=both[:, 1].rearrange("p h j d -> p h (j d)"),
-                in0=u,
-                in1=table[:, 1].unsqueeze(1).to_broadcast([P, ROPE_HEADS, ROUND * D]),
+                out=both[:, 1].rearrange("p h j (w d) -> p h j w d", w=2),
+                in0=normed[n][:].rearrange("p h j (w d) -> p h j w d", w=2)[:, :, :, ::-1, :],
+                in1=tables[n][:, 1]
+                .rearrange("p j (w d) -> p j w d", w=2)
+                .unsqueeze(1)
+                .to_broadcast([P, ROPE_HEADS, ROUND, 2, HALF]),
                 op=ALU.mult,
             )
             tiles = slice(first, first + ROUND)
             joiner = nc.vector if n == ROUNDS - 1 else nc.gpsimd
             joiner.tensor_tensor(
-                out=rotated[b][:, :, tiles, low], in0=both[:, 0, :, :, low], in1=both[:, 1, :, :, high], op=ALU.subtract
-            )
-            joiner.tensor_tensor(
-                out=rotated[b][:, :, tiles, high], in0=both[:, 0, :, :, high], in1=both[:, 1, :, :, low], op=ALU.add
+                out=rotated[b][:, :, tiles, :], in0=both[:, 0], in1=both[:, 1], op=ALU.add
             )
             if b == BATCHES - 1:
                 store(b, first, first + ROUND)
@@ -337,11 +342,11 @@ def tile_refattention_pa_t_kernel(
                 start_normalise(n + NORMALISE_LEAD)
             if n + PROJECT_LEAD < ROUNDS:
                 project_round(n + PROJECT_LEAD)
-            if n + TABLES_LEAD < ROUNDS:
-                tables_round(n + TABLES_LEAD)
             while next_transpose <= min(n + TRANSPOSE_LEAD, 2 * n + 4, ROUNDS - 1):
                 transpose_round(next_transpose)
                 next_transpose += 1
+            if n + TABLES_LEAD < ROUNDS:
+                tables_round(n + TABLES_LEAD)
             if n + PROJECT_LEAD < ROUNDS:
                 inverse_rms_round(n + PROJECT_LEAD)
             rotate_round(n)

@@ -36,7 +36,7 @@ QUANTISE_LEAD = 4
 PROJECT_LEAD = 2
 NORMALISE_LEAD = 1
 TABLES_LEAD = 1
-SHARED_ROUNDS = 3
+SHARED_ROUNDS = 1
 X_BATCHES_AHEAD = 4
 TABLE_BATCHES_AHEAD = 2
 
@@ -107,8 +107,7 @@ def tile_refattention_pa_t_kernel(
             nc.sync.dma_start(out=cos_sb[b][:], in_=cos_dram[:, tiles, :])
             nc.sync.dma_start(out=sin_sb[b][:], in_=sin_dram[:, tiles, :])
 
-        for t in range(ROUND):
-            load_x(0, t, t + 1)
+        load_x(0, 0, ROUND)
         weights = ((Wq_words, Wq_scales, 0), (Wk_words, Wk_scales, QUERY_HEADS * D), (Wv_words, Wv_scales, ROPE_HEADS * D))
         for words, scales, first_feature in weights:
             n_features = words.shape[2]
@@ -117,7 +116,6 @@ def tile_refattention_pa_t_kernel(
                 out=w_codes[:, :, byte_cols].bitcast(I32),
                 in_=words.rearrange("g p n t -> p g (n t)").bitcast(I32),
             )
-        load_x(0, ROUND, BATCH)
         for words, scales, first_feature in weights:
             cols = slice(first_feature, first_feature + words.shape[2])
             for quadrant in range(4):
@@ -142,6 +140,7 @@ def tile_refattention_pa_t_kernel(
         nc.scalar.activation(out=warm[:], in_=eps[:], func=ACT.Abs_reciprocal_sqrt)
         ident = keep.tile([P, P], F32)
         make_identity(nc, ident[:])
+        nc.gpsimd.dma_start(out=x_sb[0][:, ROUND:BATCH, :], in_=x_dram[:, ROUND:BATCH, :])
         plus_one = keep.tile([P, P], BF16)
         nc.vector.tensor_copy(out=plus_one[:], in_=ident[:])
         minus_one = keep.tile([P, P], BF16)

@@ -36,6 +36,7 @@ QUANTISE_LEAD = 4
 PROJECT_LEAD = 2
 NORMALISE_LEAD = 1
 TABLES_LEAD = 1
+SCALAR_VALUE_ROUNDS = 2
 SHARED_ROUNDS = 1
 X_BATCHES_AHEAD = 4
 TABLE_BATCHES_AHEAD = 2
@@ -125,10 +126,10 @@ def tile_refattention_pa_t_kernel(
                     .rearrange("g q n -> q g n")
                     .bitcast(I32),
                 )
+        load_x(1, 0, ROUND)
         load_tables(0)
         nc.sync.dma_start(out=q_gain[:], in_=q_norm_w.partition_broadcast(P))
         nc.sync.dma_start(out=k_gain[:], in_=k_norm_w.partition_broadcast(P))
-        load_x(1, 0, ROUND)
         load_x(1, ROUND, BATCH)
         load_x(2)
         load_tables(1)
@@ -149,6 +150,7 @@ def tile_refattention_pa_t_kernel(
         low = slice(0, HALF)
         high = slice(HALF, D)
 
+        transposed = {}
         grouped = {}
         codes = {}
         planes = {}
@@ -163,7 +165,6 @@ def tile_refattention_pa_t_kernel(
 
         def transpose_round(n):
             b, first = place(n)
-            grouped[n] = stage.tile([P, ROUND, PASSES, P, PACK], BF16, align_bytes=64, name="grouped")
             for j in range(ROUND):
                 words = x_sb[b][:, first + j, :].bitcast(F32)
                 xt = psum_t.tile([P, PASSES, 2, P], F32)
@@ -174,14 +175,21 @@ def tile_refattention_pa_t_kernel(
                             words[:, 2 * P * g + u : 2 * P * (g + 1) : 2],
                             ident[:],
                         )
+                transposed[n, j] = xt
+
+        def collect_round(n, between=None):
+            grouped[n] = stage.tile([P, ROUND, PASSES, P, PACK], BF16, align_bytes=64, name="grouped")
+            for j in range(ROUND):
                 copy_out = nc.vector.tensor_copy if n < SHARED_ROUNDS and j == 1 else nc.scalar.copy
                 copy_out(
                     out=grouped[n][:, j]
                     .rearrange("p g r t -> p (g r t)")
                     .bitcast(F32)
                     .rearrange("p (g r u) -> p g r u", g=PASSES, u=2),
-                    in_=xt[:].rearrange("p g u r -> p g r u"),
+                    in_=transposed[n, j][:].rearrange("p g u r -> p g r u"),
                 )
+                if j == 0 and between is not None:
+                    between()
 
         def quantise_round(n):
             codes[n] = keep.tile([P, ROUND, PASSES, P], U32, align_bytes=64, name="codes%d" % n)
@@ -193,7 +201,6 @@ def tile_refattention_pa_t_kernel(
             )
 
         def project_round(n):
-            square_sums[n] = small.tile([P, ROUND, HEADS], F32, name="square_sum")
             for j in range(ROUND):
                 acc = psum_o.tile([P, FEATURES], F32)
                 for g in range(PASSES):
@@ -206,27 +213,31 @@ def tile_refattention_pa_t_kernel(
                         start=(g == 0),
                         stop=(g == PASSES - 1),
                     )
+                products[n, j] = acc
+
+        def square_round(n, tiles=slice(0, ROUND)):
+            if tiles.start == 0:
+                square_sums[n] = small.tile([P, ROUND, HEADS], F32, name="square_sum")
+            for j in range(tiles.start, tiles.stop):
                 for h in range(HEADS):
                     squares = stage.tile([P, D], BF16)
                     nc.scalar.activation(
                         out=squares[:],
-                        in_=acc[:, D * h : D * (h + 1)],
+                        in_=products[n, j][:, D * h : D * (h + 1)],
                         func=ACT.Square,
                         accum_out=square_sums[n][:, j, h : h + 1],
                     )
-                products[n, j] = acc
 
-        def inverse_rms_round(n):
-            inv_rms = small.tile([P, ROUND, HEADS], F32)
+        def inverse_rms_round(n, tiles=slice(0, ROUND)):
+            if tiles.start == 0:
+                rstd[n] = small.tile([P, ROUND, HEADS], F32, name="inv_rms")
             nc.scalar.activation(
-                out=inv_rms[:].rearrange("p j h -> p (j h)"),
-                in_=square_sums[n][:].rearrange("p j h -> p (j h)"),
+                out=rstd[n][:, tiles, :].rearrange("p j h -> p (j h)"),
+                in_=square_sums[n][:, tiles, :].rearrange("p j h -> p (j h)"),
                 func=ACT.Abs_reciprocal_sqrt,
                 bias=eps[:],
                 scale=1.0 / D,
             )
-            for j in range(ROUND):
-                rstd[n, j] = inv_rms[:, j, :]
 
         def tables_round(n):
             b, first = place(n)
@@ -242,38 +253,51 @@ def tile_refattention_pa_t_kernel(
                 out=tables[n][:, 1, :, high], lhsT=plus_one[:], rhs=sin_sb[b][:, tiles, high], start=True, stop=True
             )
 
-        def normalise_round(n):
+        def normalise_round(n, tiles=slice(0, ROUND)):
             b, first = place(n)
-            normed[n] = keep.tile([P, ROPE_HEADS, ROUND, D], F32, name="normed%d" % n)
-            if first == 0:
-                value[b] = keep.tile([P, BATCH, D], F32, name="value%d" % b)
-            for j in range(ROUND):
+            if tiles.start == 0:
+                normed[n] = keep.tile([P, ROPE_HEADS, ROUND, D], F32, name="normed%d" % n)
+                if first == 0:
+                    value[b] = keep.tile([P, BATCH, D], F32, name="value%d" % b)
+            for j in range(tiles.start, tiles.stop):
                 acc = products[n, j]
                 for h in range(ROPE_HEADS):
                     nc.vector.scalar_tensor_tensor(
                         out=normed[n][:, h, j, :],
                         in0=acc[:, D * h : D * (h + 1)],
-                        scalar=rstd[n, j][:, h : h + 1],
+                        scalar=rstd[n][:, j, h : h + 1],
                         in1=gain_of_head[h][:],
                         op0=ALU.mult,
                         op1=ALU.mult,
                     )
-                nc.vector.tensor_scalar_mul(
+                if n < ROUNDS - SCALAR_VALUE_ROUNDS:
+                    nc.vector.tensor_scalar_mul(
+                        out=value[b][:, first + j, :],
+                        in0=acc[:, D * ROPE_HEADS : FEATURES],
+                        scalar1=rstd[n][:, j, ROPE_HEADS:HEADS],
+                    )
+
+        def scalar_value_round(n):
+            b, first = place(n)
+            for j in range(ROUND):
+                nc.scalar.activation(
                     out=value[b][:, first + j, :],
-                    in0=acc[:, D * ROPE_HEADS : FEATURES],
-                    scalar1=rstd[n, j][:, ROPE_HEADS : HEADS],
+                    in_=products[n, j][:, D * ROPE_HEADS : FEATURES],
+                    func=ACT.Copy,
+                    scale=rstd[n][:, j, ROPE_HEADS:HEADS],
                 )
 
-        def key_times_cos_round(n):
+        def key_times_cos_round(n, tiles=slice(0, ROUND)):
             b, first = place(n)
-            both = stage.tile([P, 2, ROPE_HEADS, ROUND, D], F32, name="both")
-            products_of[n] = both
-            nc.gpsimd.tensor_tensor(
-                out=both[:, 0, QUERY_HEADS],
-                in0=normed[n][:, QUERY_HEADS],
-                in1=cos_sb[b][:, first : first + ROUND, :],
-                op=ALU.mult,
-            )
+            if tiles.start == 0:
+                products_of[n] = stage.tile([P, 2, ROPE_HEADS, ROUND, D], F32, name="both")
+            if n < ROUNDS - 1:
+                nc.gpsimd.tensor_tensor(
+                    out=products_of[n][:, 0, QUERY_HEADS, tiles],
+                    in0=normed[n][:, QUERY_HEADS, tiles],
+                    in1=cos_sb[b][:, first + tiles.start : first + tiles.stop, :],
+                    op=ALU.mult,
+                )
 
         def store(b, start, stop):
             tiles = slice(BATCH * b + start, BATCH * b + stop)
@@ -281,74 +305,93 @@ def tile_refattention_pa_t_kernel(
             nc.sync.dma_start(out=q_dram[:, :, tiles, :], in_=rotated[b][:, 0:2, start:stop, :])
             nc.sync.dma_start(out=k_dram[:, 0, tiles, :], in_=rotated[b][:, 2, start:stop, :])
 
-        def rotate_round(n):
+        def rotate_round(n, tiles=slice(0, ROUND)):
             b, first = place(n)
             both = products_of[n]
-            if first == 0:
+            n_tiles = tiles.stop - tiles.start
+            if first == 0 and tiles.start == 0:
                 rotated[b] = results.tile([P, ROPE_HEADS, BATCH, D], F32, name="rotated")
-            u = normed[n][:].rearrange("p h j d -> p h (j d)")
-            table = tables[n][:].rearrange("p w j d -> p w (j d)")
+            heads = ROPE_HEADS if n == ROUNDS - 1 else QUERY_HEADS
             nc.vector.tensor_tensor(
-                out=both[:, 0, 0:QUERY_HEADS].rearrange("p h j d -> p h (j d)"),
-                in0=u[:, 0:QUERY_HEADS],
-                in1=table[:, 0].unsqueeze(1).to_broadcast([P, QUERY_HEADS, ROUND * D]),
+                out=both[:, 0, 0:heads, tiles],
+                in0=normed[n][:, 0:heads, tiles],
+                in1=tables[n][:, 0, tiles].unsqueeze(1).to_broadcast([P, heads, n_tiles, D]),
                 op=ALU.mult,
             )
-            nc.vector.tensor_tensor(
-                out=both[:, 1].rearrange("p h j (w d) -> p h j w d", w=2),
-                in0=normed[n][:].rearrange("p h j (w d) -> p h j w d", w=2)[:, :, :, ::-1, :],
-                in1=tables[n][:, 1]
-                .rearrange("p j (w d) -> p j w d", w=2)
-                .unsqueeze(1)
-                .to_broadcast([P, ROPE_HEADS, ROUND, 2, HALF]),
-                op=ALU.mult,
-            )
-            tiles = slice(first, first + ROUND)
+            if n_tiles == 1:
+                j = tiles.start
+                nc.vector.tensor_tensor(
+                    out=both[:, 1, :, j].rearrange("p h (w d) -> p h w d", w=2),
+                    in0=normed[n][:, :, j].rearrange("p h (w d) -> p h w d", w=2)[:, :, ::-1, :],
+                    in1=tables[n][:, 1, j]
+                    .rearrange("p (w d) -> p w d", w=2)
+                    .unsqueeze(1)
+                    .to_broadcast([P, ROPE_HEADS, 2, HALF]),
+                    op=ALU.mult,
+                )
+            else:
+                nc.vector.tensor_tensor(
+                    out=both[:, 1].rearrange("p h j (w d) -> p h j w d", w=2),
+                    in0=normed[n][:].rearrange("p h j (w d) -> p h j w d", w=2)[:, :, :, ::-1, :],
+                    in1=tables[n][:, 1]
+                    .rearrange("p j (w d) -> p j w d", w=2)
+                    .unsqueeze(1)
+                    .to_broadcast([P, ROPE_HEADS, ROUND, 2, HALF]),
+                    op=ALU.mult,
+                )
+            out_tiles = slice(first + tiles.start, first + tiles.stop)
             joiner = nc.vector if n == ROUNDS - 1 else nc.gpsimd
             joiner.tensor_tensor(
-                out=rotated[b][:, :, tiles, :], in0=both[:, 0], in1=both[:, 1], op=ALU.add
+                out=rotated[b][:, :, out_tiles, :],
+                in0=both[:, 0, :, tiles],
+                in1=both[:, 1, :, tiles],
+                op=ALU.add,
             )
             if b == BATCHES - 1:
-                store(b, first, first + ROUND)
-            elif first + ROUND == BATCH:
+                store(b, out_tiles.start, out_tiles.stop)
+            elif out_tiles.stop == BATCH:
                 store(b, 0, BATCH)
 
-        def start_normalise(n):
-            normalise_round(n)
-            key_times_cos_round(n)
-
         transpose_round(0)
+        collect_round(0)
         quantise_round(0)
         transpose_round(1)
         project_round(0)
-        inverse_rms_round(0)
-        quantise_round(1)
+        collect_round(1)
+        square_round(0)
         tables_round(0)
-        start_normalise(0)
         transpose_round(2)
+        quantise_round(1)
         project_round(1)
-        inverse_rms_round(1)
-        quantise_round(2)
-        next_transpose = 3
-        next_quantise = 3
+        collect_round(2, lambda: inverse_rms_round(0))
+        transpose_round(3)
+        next_quantise = 2
         for n in range(ROUNDS):
             b, first = place(n)
             if first == 0 and b + X_BATCHES_AHEAD < BATCHES:
                 load_x(b + X_BATCHES_AHEAD)
             if first == 0 and b + TABLE_BATCHES_AHEAD < BATCHES:
                 load_tables(b + TABLE_BATCHES_AHEAD)
-            if n + NORMALISE_LEAD < ROUNDS:
-                start_normalise(n + NORMALISE_LEAD)
-            if n + PROJECT_LEAD < ROUNDS:
-                project_round(n + PROJECT_LEAD)
-            while next_transpose <= min(n + TRANSPOSE_LEAD, 2 * n + 4, ROUNDS - 1):
-                transpose_round(next_transpose)
-                next_transpose += 1
-            if n + TABLES_LEAD < ROUNDS:
-                tables_round(n + TABLES_LEAD)
-            if n + PROJECT_LEAD < ROUNDS:
-                inverse_rms_round(n + PROJECT_LEAD)
+            normalise_round(n)
+            key_times_cos_round(n)
+            if n > 1 and n + 2 < ROUNDS:
+                project_round(n + 2)
+            if n + 1 < ROUNDS:
+                square_round(n + 1)
+            if n + 3 < ROUNDS:
+                collect_round(n + 3, lambda: inverse_rms_round(n + 1))
+            elif n + 1 < ROUNDS:
+                inverse_rms_round(n + 1)
+            if n > 1 and n + 4 < ROUNDS:
+                transpose_round(n + 4)
+            if n + 1 < ROUNDS:
+                tables_round(n + 1)
+            if n >= ROUNDS - SCALAR_VALUE_ROUNDS:
+                scalar_value_round(n)
             rotate_round(n)
-            while next_quantise <= min(n + QUANTISE_LEAD, 2 * n + 3, ROUNDS - 1):
+            while next_quantise <= min(n + 3, 2 * n + 2, ROUNDS - 1):
                 quantise_round(next_quantise)
                 next_quantise += 1
+            if n <= 1:
+                project_round(n + 2)
+                transpose_round(n + 4)

@@ -36,7 +36,6 @@ QUANTISE_LEAD = 4
 PROJECT_LEAD = 2
 NORMALISE_LEAD = 1
 TABLES_LEAD = 1
-SCALAR_VALUE_ROUNDS = 2
 SHARED_ROUNDS = 1
 X_BATCHES_AHEAD = 4
 TABLE_BATCHES_AHEAD = 2
@@ -74,6 +73,9 @@ def tile_refattention_pa_t_kernel(
         first_tile = ROUND * n
         return first_tile // BATCH, first_tile % BATCH
 
+    def scalar_values(n):
+        return [0, 1] if n >= ROUNDS - 2 else []
+
     with ExitStack() as ctx:
         ctx.enter_context(tc.manual_schedule())
         keep = ctx.enter_context(tc.tile_pool(name="keep", bufs=1))
@@ -86,6 +88,7 @@ def tile_refattention_pa_t_kernel(
         psum_c = ctx.enter_context(tc.psum_pool(name="psum_c", bufs=2))
 
         x_sb = {}
+        value = [keep.tile([P, BATCH, D], F32, name="value%d" % b) for b in range(BATCHES)]
         cos_sb = [keep.tile([P, BATCH, D], BF16, name="cos%d" % b) for b in range(BATCHES)]
         sin_sb = [keep.tile([P, BATCH, D], BF16, name="sin%d" % b) for b in range(BATCHES)]
         q_gain = keep.tile([P, D], BF16)
@@ -111,13 +114,6 @@ def tile_refattention_pa_t_kernel(
         load_x(0, 0, ROUND)
         weights = ((Wq_words, Wq_scales, 0), (Wk_words, Wk_scales, QUERY_HEADS * D), (Wv_words, Wv_scales, ROPE_HEADS * D))
         for words, scales, first_feature in weights:
-            n_features = words.shape[2]
-            byte_cols = slice(PACK * first_feature, PACK * (first_feature + n_features))
-            nc.sync.dma_start(
-                out=w_codes[:, :, byte_cols].bitcast(I32),
-                in_=words.rearrange("g p n t -> p g (n t)").bitcast(I32),
-            )
-        for words, scales, first_feature in weights:
             cols = slice(first_feature, first_feature + words.shape[2])
             for quadrant in range(4):
                 nc.sync.dma_start(
@@ -126,6 +122,13 @@ def tile_refattention_pa_t_kernel(
                     .rearrange("g q n -> q g n")
                     .bitcast(I32),
                 )
+        for words, scales, first_feature in weights:
+            n_features = words.shape[2]
+            byte_cols = slice(PACK * first_feature, PACK * (first_feature + n_features))
+            nc.sync.dma_start(
+                out=w_codes[:, :, byte_cols].bitcast(I32),
+                in_=words.rearrange("g p n t -> p g (n t)").bitcast(I32),
+            )
         load_x(1, 0, ROUND)
         load_tables(0)
         nc.sync.dma_start(out=q_gain[:], in_=q_norm_w.partition_broadcast(P))
@@ -161,7 +164,6 @@ def tile_refattention_pa_t_kernel(
         tables = {}
         products_of = {}
         rotated = {}
-        value = {}
 
         def transpose_round(n):
             b, first = place(n)
@@ -191,14 +193,16 @@ def tile_refattention_pa_t_kernel(
                 if j == 0 and between is not None:
                     between()
 
-        def quantise_round(n):
-            codes[n] = keep.tile([P, ROUND, PASSES, P], U32, align_bytes=64, name="codes%d" % n)
-            planes[n] = keep.tile([P, ROUND, PASSES, P], U8, align_bytes=64, name="planes%d" % n)
-            nc.vector.quantize_mx(
-                out=codes[n][:].rearrange("p j g r -> p (j g r)").bitcast(FP8X4),
-                scales=planes[n][:].rearrange("p j g r -> p (j g r)"),
-                in_=grouped[n][:].rearrange("p j g r t -> p (j g r t)"),
-            )
+        def quantise_round(n, tiles=range(ROUND)):
+            if 0 in tiles:
+                codes[n] = keep.tile([P, ROUND, PASSES, P], U32, align_bytes=64, name="codes%d" % n)
+                planes[n] = keep.tile([P, ROUND, PASSES, P], U8, align_bytes=64, name="planes%d" % n)
+            for j in tiles:
+                nc.vector.quantize_mx(
+                    out=codes[n][:, j].rearrange("p g r -> p (g r)").bitcast(FP8X4),
+                    scales=planes[n][:, j].rearrange("p g r -> p (g r)"),
+                    in_=grouped[n][:, j].rearrange("p g r t -> p (g r t)"),
+                )
 
         def project_round(n):
             for j in range(ROUND):
@@ -257,8 +261,6 @@ def tile_refattention_pa_t_kernel(
             b, first = place(n)
             if tiles.start == 0:
                 normed[n] = keep.tile([P, ROPE_HEADS, ROUND, D], F32, name="normed%d" % n)
-                if first == 0:
-                    value[b] = keep.tile([P, BATCH, D], F32, name="value%d" % b)
             for j in range(tiles.start, tiles.stop):
                 acc = products[n, j]
                 for h in range(ROPE_HEADS):
@@ -270,7 +272,7 @@ def tile_refattention_pa_t_kernel(
                         op0=ALU.mult,
                         op1=ALU.mult,
                     )
-                if n < ROUNDS - SCALAR_VALUE_ROUNDS:
+                if j not in scalar_values(n):
                     nc.vector.tensor_scalar_mul(
                         out=value[b][:, first + j, :],
                         in0=acc[:, D * ROPE_HEADS : FEATURES],
@@ -279,7 +281,7 @@ def tile_refattention_pa_t_kernel(
 
         def scalar_value_round(n):
             b, first = place(n)
-            for j in range(ROUND):
+            for j in scalar_values(n):
                 nc.scalar.activation(
                     out=value[b][:, first + j, :],
                     in_=products[n, j][:, D * ROPE_HEADS : FEATURES],
@@ -305,7 +307,7 @@ def tile_refattention_pa_t_kernel(
             nc.sync.dma_start(out=q_dram[:, :, tiles, :], in_=rotated[b][:, 0:2, start:stop, :])
             nc.sync.dma_start(out=k_dram[:, 0, tiles, :], in_=rotated[b][:, 2, start:stop, :])
 
-        def rotate_round(n, tiles=slice(0, ROUND)):
+        def rotate_round(n, tiles=slice(0, ROUND), between=None):
             b, first = place(n)
             both = products_of[n]
             n_tiles = tiles.stop - tiles.start
@@ -318,6 +320,8 @@ def tile_refattention_pa_t_kernel(
                 in1=tables[n][:, 0, tiles].unsqueeze(1).to_broadcast([P, heads, n_tiles, D]),
                 op=ALU.mult,
             )
+            if between is not None:
+                between()
             if n_tiles == 1:
                 j = tiles.start
                 nc.vector.tensor_tensor(
@@ -359,11 +363,12 @@ def tile_refattention_pa_t_kernel(
         project_round(0)
         collect_round(1)
         square_round(0)
+        inverse_rms_round(0)
         tables_round(0)
         transpose_round(2)
         quantise_round(1)
         project_round(1)
-        collect_round(2, lambda: inverse_rms_round(0))
+        collect_round(2)
         transpose_round(3)
         next_quantise = 2
         for n in range(ROUNDS):
@@ -372,9 +377,12 @@ def tile_refattention_pa_t_kernel(
                 load_x(b + X_BATCHES_AHEAD)
             if first == 0 and b + TABLE_BATCHES_AHEAD < BATCHES:
                 load_tables(b + TABLE_BATCHES_AHEAD)
+            if n < ROUNDS - 2:
+                scalar_value_round(n)
             normalise_round(n)
             key_times_cos_round(n)
-            if n > 1 and n + 2 < ROUNDS:
+            early = n + 2 < next_quantise
+            if early and n + 2 < ROUNDS:
                 project_round(n + 2)
             if n + 1 < ROUNDS:
                 square_round(n + 1)
@@ -382,16 +390,19 @@ def tile_refattention_pa_t_kernel(
                 collect_round(n + 3, lambda: inverse_rms_round(n + 1))
             elif n + 1 < ROUNDS:
                 inverse_rms_round(n + 1)
-            if n > 1 and n + 4 < ROUNDS:
+            if early and n + 4 < ROUNDS:
                 transpose_round(n + 4)
             if n + 1 < ROUNDS:
                 tables_round(n + 1)
-            if n >= ROUNDS - SCALAR_VALUE_ROUNDS:
+            if n >= ROUNDS - 2:
                 scalar_value_round(n)
-            rotate_round(n)
-            while next_quantise <= min(n + 3, 2 * n + 2, ROUNDS - 1):
-                quantise_round(next_quantise)
+            if n + 2 < ROUNDS:
+                rotate_round(n, between=lambda: quantise_round(n + 2, [0]))
+                quantise_round(n + 2, [1])
                 next_quantise += 1
-            if n <= 1:
+            else:
+                rotate_round(n)
+            if not early and n + 2 < ROUNDS:
                 project_round(n + 2)
-                transpose_round(n + 4)
+                if n + 4 < ROUNDS:
+                    transpose_round(n + 4)

@@ -193,11 +193,10 @@ def tile_refattention_pa_t_kernel(
                 if j == 0 and between is not None:
                     between()
 
-        def quantise_round(n, tiles=range(ROUND)):
-            if 0 in tiles:
-                codes[n] = keep.tile([P, ROUND, PASSES, P], U32, align_bytes=64, name="codes%d" % n)
-                planes[n] = keep.tile([P, ROUND, PASSES, P], U8, align_bytes=64, name="planes%d" % n)
-            for j in tiles:
+        def quantise_round(n):
+            codes[n] = keep.tile([P, ROUND, PASSES, P], U32, align_bytes=64, name="codes%d" % n)
+            planes[n] = keep.tile([P, ROUND, PASSES, P], U8, align_bytes=64, name="planes%d" % n)
+            for j in range(ROUND):
                 nc.vector.quantize_mx(
                     out=codes[n][:, j].rearrange("p g r -> p (g r)").bitcast(FP8X4),
                     scales=planes[n][:, j].rearrange("p g r -> p (g r)"),
@@ -307,7 +306,7 @@ def tile_refattention_pa_t_kernel(
             nc.sync.dma_start(out=q_dram[:, :, tiles, :], in_=rotated[b][:, 0:2, start:stop, :])
             nc.sync.dma_start(out=k_dram[:, 0, tiles, :], in_=rotated[b][:, 2, start:stop, :])
 
-        def rotate_round(n, tiles=slice(0, ROUND), between=None):
+        def rotate_round(n, tiles=slice(0, ROUND)):
             b, first = place(n)
             both = products_of[n]
             n_tiles = tiles.stop - tiles.start
@@ -320,8 +319,6 @@ def tile_refattention_pa_t_kernel(
                 in1=tables[n][:, 0, tiles].unsqueeze(1).to_broadcast([P, heads, n_tiles, D]),
                 op=ALU.mult,
             )
-            if between is not None:
-                between()
             if n_tiles == 1:
                 j = tiles.start
                 nc.vector.tensor_tensor(
@@ -386,22 +383,19 @@ def tile_refattention_pa_t_kernel(
                 project_round(n + 2)
             if n + 1 < ROUNDS:
                 square_round(n + 1)
-            if n + 3 < ROUNDS:
-                collect_round(n + 3, lambda: inverse_rms_round(n + 1))
-            elif n + 1 < ROUNDS:
                 inverse_rms_round(n + 1)
+            if n + 3 < ROUNDS:
+                collect_round(n + 3)
             if early and n + 4 < ROUNDS:
                 transpose_round(n + 4)
             if n + 1 < ROUNDS:
                 tables_round(n + 1)
             if n >= ROUNDS - 2:
                 scalar_value_round(n)
-            if n + 2 < ROUNDS:
-                rotate_round(n, between=lambda: quantise_round(n + 2, [0]))
-                quantise_round(n + 2, [1])
+            rotate_round(n)
+            while next_quantise <= min(n + (3 if n >= 99 else 2), ROUNDS - 1):
+                quantise_round(next_quantise)
                 next_quantise += 1
-            else:
-                rotate_round(n)
             if not early and n + 2 < ROUNDS:
                 project_round(n + 2)
                 if n + 4 < ROUNDS:

@@ -24,21 +24,26 @@ HEADS = 4
 ROPE_HEADS = 3
 QUERY_HEADS = 2
 FEATURES = HEADS * D
+QUERIES = slice(0, QUERY_HEADS)
+KEY = slice(QUERY_HEADS, ROPE_HEADS)
+ALL_ROPE = slice(0, ROPE_HEADS)
 TILES = TOKENS // P
 BATCH = 4
 BATCHES = TILES // BATCH
 ROUND = 2
 ROUNDS = TILES // ROUND
+LAST = ROUNDS - 1
 EPS = 1e-6
 
-TRANSPOSE_LEAD = 5
-QUANTISE_LEAD = 4
+TRANSPOSE_LEAD = 4
+COLLECT_LEAD = 3
+QUANTISE_LEAD = 2
 PROJECT_LEAD = 2
-NORMALISE_LEAD = 1
+SQUARE_LEAD = 1
 TABLES_LEAD = 1
-SHARED_ROUNDS = 1
 X_BATCHES_AHEAD = 4
 TABLE_BATCHES_AHEAD = 2
+SCALAR_VALUE_ROUNDS = 2
 
 FLOPS = 2 * TOKENS * HID * FEATURES
 
@@ -69,25 +74,26 @@ def tile_refattention_pa_t_kernel(
     k_dram = out_1.rearrange("b h (p t) d -> p (b h) t d", t=TILES)
     v_dram = out_2.rearrange("b h (p t) d -> p (b h) t d", t=TILES)
 
+    low = slice(0, HALF)
+    high = slice(HALF, D)
+    both_tiles = slice(0, ROUND)
+    single_tiles = tuple(slice(j, j + 1) for j in range(ROUND))
+
     def place(n):
         first_tile = ROUND * n
         return first_tile // BATCH, first_tile % BATCH
-
-    def scalar_values(n):
-        return [0, 1] if n >= ROUNDS - 2 else []
 
     with ExitStack() as ctx:
         ctx.enter_context(tc.manual_schedule())
         keep = ctx.enter_context(tc.tile_pool(name="keep", bufs=1))
         stage = ctx.enter_context(tc.tile_pool(name="stage", bufs=4))
         small = ctx.enter_context(tc.tile_pool(name="small", bufs=4 * ROUND))
-        inputs = ctx.enter_context(tc.tile_pool(name="inputs", bufs=5))
+        inputs = ctx.enter_context(tc.tile_pool(name="inputs", bufs=1 + X_BATCHES_AHEAD))
         results = ctx.enter_context(tc.tile_pool(name="results", bufs=3))
         psum_t = ctx.enter_context(tc.psum_pool(name="psum_t", bufs=ROUND))
         psum_o = ctx.enter_context(tc.psum_pool(name="psum_o", bufs=2 * ROUND))
         psum_c = ctx.enter_context(tc.psum_pool(name="psum_c", bufs=2))
 
-        x_sb = {}
         value = [keep.tile([P, BATCH, D], F32, name="value%d" % b) for b in range(BATCHES)]
         cos_sb = [keep.tile([P, BATCH, D], BF16, name="cos%d" % b) for b in range(BATCHES)]
         sin_sb = [keep.tile([P, BATCH, D], BF16, name="sin%d" % b) for b in range(BATCHES)]
@@ -98,6 +104,19 @@ def tile_refattention_pa_t_kernel(
         w_codes = keep.tile([P, PASSES, PACK * FEATURES], U8, align_bytes=64)
         w_planes = keep.tile([P, PASSES, FEATURES], U8, align_bytes=64)
         nc.vector.memset(w_planes[:].rearrange("p g n -> p (g n)").bitcast(I32), 0)
+
+        x_sb = {}
+        transposed = {}
+        grouped = {}
+        codes = {}
+        planes = {}
+        products = {}
+        square_sums = {}
+        rstd = {}
+        normed = {}
+        tables = {}
+        rope_products = {}
+        rotated = {}
 
         def load_x(b, start=0, stop=BATCH):
             if start == 0:
@@ -112,7 +131,11 @@ def tile_refattention_pa_t_kernel(
             nc.sync.dma_start(out=sin_sb[b][:], in_=sin_dram[:, tiles, :])
 
         load_x(0, 0, ROUND)
-        weights = ((Wq_words, Wq_scales, 0), (Wk_words, Wk_scales, QUERY_HEADS * D), (Wv_words, Wv_scales, ROPE_HEADS * D))
+        weights = (
+            (Wq_words, Wq_scales, 0),
+            (Wk_words, Wk_scales, QUERY_HEADS * D),
+            (Wv_words, Wv_scales, ROPE_HEADS * D),
+        )
         for words, scales, first_feature in weights:
             cols = slice(first_feature, first_feature + words.shape[2])
             for quadrant in range(4):
@@ -123,8 +146,7 @@ def tile_refattention_pa_t_kernel(
                     .bitcast(I32),
                 )
         for words, scales, first_feature in weights:
-            n_features = words.shape[2]
-            byte_cols = slice(PACK * first_feature, PACK * (first_feature + n_features))
+            byte_cols = slice(PACK * first_feature, PACK * (first_feature + words.shape[2]))
             nc.sync.dma_start(
                 out=w_codes[:, :, byte_cols].bitcast(I32),
                 in_=words.rearrange("g p n t -> p g (n t)").bitcast(I32),
@@ -150,21 +172,6 @@ def tile_refattention_pa_t_kernel(
         minus_one = keep.tile([P, P], BF16)
         nc.vector.tensor_scalar_mul(out=minus_one[:], in0=ident[:], scalar1=-1.0)
 
-        low = slice(0, HALF)
-        high = slice(HALF, D)
-
-        transposed = {}
-        grouped = {}
-        codes = {}
-        planes = {}
-        products = {}
-        square_sums = {}
-        rstd = {}
-        normed = {}
-        tables = {}
-        products_of = {}
-        rotated = {}
-
         def transpose_round(n):
             b, first = place(n)
             for j in range(ROUND):
@@ -179,10 +186,10 @@ def tile_refattention_pa_t_kernel(
                         )
                 transposed[n, j] = xt
 
-        def collect_round(n, between=None):
+        def collect_round(n):
             grouped[n] = stage.tile([P, ROUND, PASSES, P, PACK], BF16, align_bytes=64, name="grouped")
             for j in range(ROUND):
-                copy_out = nc.vector.tensor_copy if n < SHARED_ROUNDS and j == 1 else nc.scalar.copy
+                copy_out = nc.vector.tensor_copy if (n, j) == (0, 1) else nc.scalar.copy
                 copy_out(
                     out=grouped[n][:, j]
                     .rearrange("p g r t -> p (g r t)")
@@ -190,8 +197,6 @@ def tile_refattention_pa_t_kernel(
                     .rearrange("p (g r u) -> p g r u", g=PASSES, u=2),
                     in_=transposed[n, j][:].rearrange("p g u r -> p g r u"),
                 )
-                if j == 0 and between is not None:
-                    between()
 
         def quantise_round(n):
             codes[n] = keep.tile([P, ROUND, PASSES, P], U32, align_bytes=64, name="codes%d" % n)
@@ -218,7 +223,7 @@ def tile_refattention_pa_t_kernel(
                     )
                 products[n, j] = acc
 
-        def square_round(n, tiles=slice(0, ROUND)):
+        def square_round(n, tiles):
             if tiles.start == 0:
                 square_sums[n] = small.tile([P, ROUND, HEADS], F32, name="square_sum")
             for j in range(tiles.start, tiles.stop):
@@ -231,7 +236,7 @@ def tile_refattention_pa_t_kernel(
                         accum_out=square_sums[n][:, j, h : h + 1],
                     )
 
-        def inverse_rms_round(n, tiles=slice(0, ROUND)):
+        def inverse_rms_round(n, tiles):
             if tiles.start == 0:
                 rstd[n] = small.tile([P, ROUND, HEADS], F32, name="inv_rms")
             nc.scalar.activation(
@@ -256,11 +261,10 @@ def tile_refattention_pa_t_kernel(
                 out=tables[n][:, 1, :, high], lhsT=plus_one[:], rhs=sin_sb[b][:, tiles, high], start=True, stop=True
             )
 
-        def normalise_round(n, tiles=slice(0, ROUND)):
+        def normalise_round(n):
             b, first = place(n)
-            if tiles.start == 0:
-                normed[n] = keep.tile([P, ROPE_HEADS, ROUND, D], F32, name="normed%d" % n)
-            for j in range(tiles.start, tiles.stop):
+            normed[n] = keep.tile([P, ROPE_HEADS, ROUND, D], F32, name="normed%d" % n)
+            for j in range(ROUND):
                 acc = products[n, j]
                 for h in range(ROPE_HEADS):
                     nc.vector.scalar_tensor_tensor(
@@ -271,7 +275,7 @@ def tile_refattention_pa_t_kernel(
                         op0=ALU.mult,
                         op1=ALU.mult,
                     )
-                if j not in scalar_values(n):
+                if n < ROUNDS - SCALAR_VALUE_ROUNDS:
                     nc.vector.tensor_scalar_mul(
                         out=value[b][:, first + j, :],
                         in0=acc[:, D * ROPE_HEADS : FEATURES],
@@ -280,7 +284,7 @@ def tile_refattention_pa_t_kernel(
 
         def scalar_value_round(n):
             b, first = place(n)
-            for j in scalar_values(n):
+            for j in range(ROUND):
                 nc.scalar.activation(
                     out=value[b][:, first + j, :],
                     in_=products[n, j][:, D * ROPE_HEADS : FEATURES],
@@ -288,70 +292,75 @@ def tile_refattention_pa_t_kernel(
                     scale=rstd[n][:, j, ROPE_HEADS:HEADS],
                 )
 
-        def key_times_cos_round(n, tiles=slice(0, ROUND)):
+        def key_times_cos_round(n):
             b, first = place(n)
-            if tiles.start == 0:
-                products_of[n] = stage.tile([P, 2, ROPE_HEADS, ROUND, D], F32, name="both")
-            if n < ROUNDS - 1:
-                nc.gpsimd.tensor_tensor(
-                    out=products_of[n][:, 0, QUERY_HEADS, tiles],
-                    in0=normed[n][:, QUERY_HEADS, tiles],
-                    in1=cos_sb[b][:, first + tiles.start : first + tiles.stop, :],
-                    op=ALU.mult,
-                )
-
-        def store(b, start, stop):
-            tiles = slice(BATCH * b + start, BATCH * b + stop)
-            nc.sync.dma_start(out=v_dram[:, 0, tiles, :], in_=value[b][:, start:stop, :])
-            nc.sync.dma_start(out=q_dram[:, :, tiles, :], in_=rotated[b][:, 0:2, start:stop, :])
-            nc.sync.dma_start(out=k_dram[:, 0, tiles, :], in_=rotated[b][:, 2, start:stop, :])
-
-        def rotate_round(n, tiles=slice(0, ROUND)):
-            b, first = place(n)
-            both = products_of[n]
-            n_tiles = tiles.stop - tiles.start
-            if first == 0 and tiles.start == 0:
-                rotated[b] = results.tile([P, ROPE_HEADS, BATCH, D], F32, name="rotated")
-            heads = ROPE_HEADS if n == ROUNDS - 1 else QUERY_HEADS
-            nc.vector.tensor_tensor(
-                out=both[:, 0, 0:heads, tiles],
-                in0=normed[n][:, 0:heads, tiles],
-                in1=tables[n][:, 0, tiles].unsqueeze(1).to_broadcast([P, heads, n_tiles, D]),
+            nc.gpsimd.tensor_tensor(
+                out=rope_products[n][:, 0, QUERY_HEADS],
+                in0=normed[n][:, QUERY_HEADS],
+                in1=cos_sb[b][:, first : first + ROUND, :],
                 op=ALU.mult,
             )
-            if n_tiles == 1:
-                j = tiles.start
-                nc.vector.tensor_tensor(
-                    out=both[:, 1, :, j].rearrange("p h (w d) -> p h w d", w=2),
-                    in0=normed[n][:, :, j].rearrange("p h (w d) -> p h w d", w=2)[:, :, ::-1, :],
-                    in1=tables[n][:, 1, j]
-                    .rearrange("p (w d) -> p w d", w=2)
-                    .unsqueeze(1)
-                    .to_broadcast([P, ROPE_HEADS, 2, HALF]),
-                    op=ALU.mult,
-                )
-            else:
-                nc.vector.tensor_tensor(
-                    out=both[:, 1].rearrange("p h j (w d) -> p h j w d", w=2),
-                    in0=normed[n][:].rearrange("p h j (w d) -> p h j w d", w=2)[:, :, :, ::-1, :],
-                    in1=tables[n][:, 1]
-                    .rearrange("p j (w d) -> p j w d", w=2)
-                    .unsqueeze(1)
-                    .to_broadcast([P, ROPE_HEADS, ROUND, 2, HALF]),
-                    op=ALU.mult,
-                )
-            out_tiles = slice(first + tiles.start, first + tiles.stop)
-            joiner = nc.vector if n == ROUNDS - 1 else nc.gpsimd
-            joiner.tensor_tensor(
-                out=rotated[b][:, :, out_tiles, :],
-                in0=both[:, 0, :, tiles],
-                in1=both[:, 1, :, tiles],
+
+        def store_values(b, tiles):
+            dram_tiles = slice(BATCH * b + tiles.start, BATCH * b + tiles.stop)
+            nc.sync.dma_start(out=v_dram[:, 0, dram_tiles, :], in_=value[b][:, tiles, :])
+
+        def store_queries(b, tiles):
+            dram_tiles = slice(BATCH * b + tiles.start, BATCH * b + tiles.stop)
+            nc.sync.dma_start(out=q_dram[:, :, dram_tiles, :], in_=rotated[b][:, QUERIES, tiles, :])
+
+        def store_key(b, tiles):
+            dram_tiles = slice(BATCH * b + tiles.start, BATCH * b + tiles.stop)
+            nc.sync.dma_start(out=k_dram[:, 0, dram_tiles, :], in_=rotated[b][:, QUERY_HEADS, tiles, :])
+
+        def store_all(b, tiles):
+            store_values(b, tiles)
+            store_queries(b, tiles)
+            store_key(b, tiles)
+
+        def multiply_round(n):
+            both = rope_products[n]
+            heads = ROPE_HEADS if n == LAST else QUERY_HEADS
+            nc.vector.tensor_tensor(
+                out=both[:, 0, 0:heads],
+                in0=normed[n][:, 0:heads],
+                in1=tables[n][:, 0].unsqueeze(1).to_broadcast([P, heads, ROUND, D]),
+                op=ALU.mult,
+            )
+            nc.vector.tensor_tensor(
+                out=both[:, 1].rearrange("p h j (w d) -> p h j w d", w=2),
+                in0=normed[n][:].rearrange("p h j (w d) -> p h j w d", w=2)[:, :, :, ::-1, :],
+                in1=tables[n][:, 1]
+                .rearrange("p j (w d) -> p j w d", w=2)
+                .unsqueeze(1)
+                .to_broadcast([P, ROPE_HEADS, ROUND, 2, HALF]),
+                op=ALU.mult,
+            )
+
+        def join_round(engine, n, heads):
+            b, first = place(n)
+            engine.tensor_tensor(
+                out=rotated[b][:, heads, first : first + ROUND, :],
+                in0=rope_products[n][:, 0, heads],
+                in1=rope_products[n][:, 1, heads],
                 op=ALU.add,
             )
-            if b == BATCHES - 1:
-                store(b, out_tiles.start, out_tiles.stop)
-            elif out_tiles.stop == BATCH:
-                store(b, 0, BATCH)
+
+        def finish_round(n):
+            b, first = place(n)
+            tiles = slice(first, first + ROUND)
+            if n < LAST:
+                join_round(nc.gpsimd, n, ALL_ROPE)
+                if n == LAST - 1:
+                    store_all(b, tiles)
+                elif tiles.stop == BATCH:
+                    store_all(b, slice(0, BATCH))
+            else:
+                store_values(b, tiles)
+                join_round(nc.vector, n, QUERIES)
+                store_queries(b, tiles)
+                join_round(nc.vector, n, KEY)
+                store_key(b, tiles)
 
         transpose_round(0)
         collect_round(0)
@@ -359,44 +368,41 @@ def tile_refattention_pa_t_kernel(
         transpose_round(1)
         project_round(0)
         collect_round(1)
-        square_round(0)
-        inverse_rms_round(0)
+        square_round(0, both_tiles)
+        inverse_rms_round(0, both_tiles)
         tables_round(0)
         transpose_round(2)
         quantise_round(1)
         project_round(1)
         collect_round(2)
         transpose_round(3)
-        next_quantise = 2
         for n in range(ROUNDS):
             b, first = place(n)
-            if first == 0 and b + X_BATCHES_AHEAD < BATCHES:
-                load_x(b + X_BATCHES_AHEAD)
-            if first == 0 and b + TABLE_BATCHES_AHEAD < BATCHES:
-                load_tables(b + TABLE_BATCHES_AHEAD)
-            if n < ROUNDS - 2:
-                scalar_value_round(n)
+            if first == 0:
+                if b + X_BATCHES_AHEAD < BATCHES:
+                    load_x(b + X_BATCHES_AHEAD)
+                if b + TABLE_BATCHES_AHEAD < BATCHES:
+                    load_tables(b + TABLE_BATCHES_AHEAD)
+                rotated[b] = results.tile([P, ROPE_HEADS, BATCH, D], F32, name="rotated")
             normalise_round(n)
-            key_times_cos_round(n)
-            early = n + 2 < next_quantise
-            if early and n + 2 < ROUNDS:
-                project_round(n + 2)
-            if n + 1 < ROUNDS:
-                square_round(n + 1)
-                inverse_rms_round(n + 1)
-            if n + 3 < ROUNDS:
-                collect_round(n + 3)
-            if early and n + 4 < ROUNDS:
-                transpose_round(n + 4)
-            if n + 1 < ROUNDS:
-                tables_round(n + 1)
-            if n >= ROUNDS - 2:
+            rope_products[n] = stage.tile([P, 2, ROPE_HEADS, ROUND, D], F32, name="rope_products")
+            if n < LAST:
+                key_times_cos_round(n)
+            if n + SQUARE_LEAD <= LAST:
+                for tiles in single_tiles if n + SQUARE_LEAD == LAST else (both_tiles,):
+                    square_round(n + SQUARE_LEAD, tiles)
+                    inverse_rms_round(n + SQUARE_LEAD, tiles)
+            if n + COLLECT_LEAD <= LAST:
+                collect_round(n + COLLECT_LEAD)
+            if n + TABLES_LEAD <= LAST:
+                tables_round(n + TABLES_LEAD)
+            if n >= ROUNDS - SCALAR_VALUE_ROUNDS:
                 scalar_value_round(n)
-            rotate_round(n)
-            while next_quantise <= min(n + (3 if n >= 99 else 2), ROUNDS - 1):
-                quantise_round(next_quantise)
-                next_quantise += 1
-            if not early and n + 2 < ROUNDS:
-                project_round(n + 2)
-                if n + 4 < ROUNDS:
-                    transpose_round(n + 4)
+            multiply_round(n)
+            finish_round(n)
+            if n + QUANTISE_LEAD <= LAST:
+                quantise_round(n + QUANTISE_LEAD)
+            if n + PROJECT_LEAD <= LAST:
+                project_round(n + PROJECT_LEAD)
+            if n + TRANSPOSE_LEAD <= LAST:
+                transpose_round(n + TRANSPOSE_LEAD)

from contextlib import ExitStack

import concourse.mybir as mybir
from concourse.masks import make_identity

F32 = mybir.dt.float32
BF16 = mybir.dt.bfloat16
I32 = mybir.dt.int32
U32 = mybir.dt.uint32
U8 = mybir.dt.uint8
FP8X4 = mybir.dt.float8_e4m3fn_x4
ACT = mybir.ActivationFunctionType
ALU = mybir.AluOpType

P = 128
PACK = 4
K_PASS = P * PACK
TOKENS = 4096
HID = 1024
PASSES = HID // K_PASS
D = 128
HALF = D // 2
HEADS = 4
ROPE_HEADS = 3
QUERY_HEADS = 2
FEATURES = HEADS * D
QUERIES = slice(0, QUERY_HEADS)
KEY = slice(QUERY_HEADS, ROPE_HEADS)
ALL_ROPE = slice(0, ROPE_HEADS)
TILES = TOKENS // P
BATCH = 4
BATCHES = TILES // BATCH
ROUND = 2
ROUNDS = TILES // ROUND
LAST = ROUNDS - 1
EPS = 1e-6

TRANSPOSE_LEAD = 4
COLLECT_LEAD = 3
QUANTISE_LEAD = 2
PROJECT_LEAD = 2
SQUARE_LEAD = 1
TABLES_LEAD = 1
X_BATCHES_AHEAD = 4
TABLE_BATCHES_AHEAD = 2
SCALAR_VALUE_ROUNDS = 2

FLOPS = 2 * TOKENS * HID * FEATURES


def tile_refattention_pa_t_kernel(
    tc,
    hidden_states,
    cos,
    sin,
    Wq_words,
    Wq_scales,
    Wk_words,
    Wk_scales,
    Wv_words,
    Wv_scales,
    q_norm_w,
    k_norm_w,
    out_0,
    out_1,
    out_2,
):
    nc = tc.nc

    x_dram = hidden_states.rearrange("b (p t) k -> p (b t) k", t=TILES)
    cos_dram = cos.rearrange("b (p t) d -> p (b t) d", t=TILES)
    sin_dram = sin.rearrange("b (p t) d -> p (b t) d", t=TILES)
    q_dram = out_0.rearrange("b h (p t) d -> p (b h) t d", t=TILES)
    k_dram = out_1.rearrange("b h (p t) d -> p (b h) t d", t=TILES)
    v_dram = out_2.rearrange("b h (p t) d -> p (b h) t d", t=TILES)

    low = slice(0, HALF)
    high = slice(HALF, D)
    both_tiles = slice(0, ROUND)
    single_tiles = tuple(slice(j, j + 1) for j in range(ROUND))

    def place(n):
        first_tile = ROUND * n
        return first_tile // BATCH, first_tile % BATCH

    with ExitStack() as ctx:
        ctx.enter_context(tc.manual_schedule())
        keep = ctx.enter_context(tc.tile_pool(name="keep", bufs=1))
        stage = ctx.enter_context(tc.tile_pool(name="stage", bufs=4))
        small = ctx.enter_context(tc.tile_pool(name="small", bufs=4 * ROUND))
        inputs = ctx.enter_context(tc.tile_pool(name="inputs", bufs=1 + X_BATCHES_AHEAD))
        results = ctx.enter_context(tc.tile_pool(name="results", bufs=3))
        psum_t = ctx.enter_context(tc.psum_pool(name="psum_t", bufs=ROUND))
        psum_o = ctx.enter_context(tc.psum_pool(name="psum_o", bufs=2 * ROUND))
        psum_c = ctx.enter_context(tc.psum_pool(name="psum_c", bufs=2))

        value = [keep.tile([P, BATCH, D], F32, name="value%d" % b) for b in range(BATCHES)]
        cos_sb = [keep.tile([P, BATCH, D], BF16, name="cos%d" % b) for b in range(BATCHES)]
        sin_sb = [keep.tile([P, BATCH, D], BF16, name="sin%d" % b) for b in range(BATCHES)]
        q_gain = keep.tile([P, D], BF16)
        k_gain = keep.tile([P, D], BF16)
        gain_of_head = (q_gain, q_gain, k_gain)

        w_codes = keep.tile([P, PASSES, PACK * FEATURES], U8, align_bytes=64)
        w_planes = keep.tile([P, PASSES, FEATURES], U8, align_bytes=64)
        nc.vector.memset(w_planes[:].rearrange("p g n -> p (g n)").bitcast(I32), 0)

        x_sb = {}
        transposed = {}
        grouped = {}
        codes = {}
        planes = {}
        products = {}
        square_sums = {}
        rstd = {}
        normed = {}
        tables = {}
        rope_products = {}
        rotated = {}

        def load_x(b, start=0, stop=BATCH):
            if start == 0:
                x_sb[b] = inputs.tile([P, BATCH, HID], BF16, name="x")
            nc.sync.dma_start(
                out=x_sb[b][:, start:stop, :], in_=x_dram[:, BATCH * b + start : BATCH * b + stop, :]
            )

        def load_tables(b):
            tiles = slice(BATCH * b, BATCH * (b + 1))
            nc.sync.dma_start(out=cos_sb[b][:], in_=cos_dram[:, tiles, :])
            nc.sync.dma_start(out=sin_sb[b][:], in_=sin_dram[:, tiles, :])

        load_x(0, 0, ROUND)
        weights = (
            (Wq_words, Wq_scales, 0),
            (Wk_words, Wk_scales, QUERY_HEADS * D),
            (Wv_words, Wv_scales, ROPE_HEADS * D),
        )
        for words, scales, first_feature in weights:
            cols = slice(first_feature, first_feature + words.shape[2])
            for quadrant in range(4):
                nc.sync.dma_start(
                    out=w_planes[32 * quadrant : 32 * quadrant + 4, :, cols].bitcast(I32),
                    in_=scales[:, 4 * quadrant : 4 * quadrant + 4, :]
                    .rearrange("g q n -> q g n")
                    .bitcast(I32),
                )
        for words, scales, first_feature in weights:
            byte_cols = slice(PACK * first_feature, PACK * (first_feature + words.shape[2]))
            nc.sync.dma_start(
                out=w_codes[:, :, byte_cols].bitcast(I32),
                in_=words.rearrange("g p n t -> p g (n t)").bitcast(I32),
            )
        load_x(1, 0, ROUND)
        load_tables(0)
        nc.sync.dma_start(out=q_gain[:], in_=q_norm_w.partition_broadcast(P))
        nc.sync.dma_start(out=k_gain[:], in_=k_norm_w.partition_broadcast(P))
        load_x(1, ROUND, BATCH)
        load_x(2)
        load_tables(1)
        load_x(3)

        eps = keep.tile([P, 1], F32)
        nc.vector.memset(eps[:], EPS)
        warm = keep.tile([P, 1], F32)
        nc.scalar.activation(out=warm[:], in_=eps[:], func=ACT.Abs_reciprocal_sqrt)
        ident = keep.tile([P, P], F32)
        make_identity(nc, ident[:])
        nc.gpsimd.dma_start(out=x_sb[0][:, ROUND:BATCH, :], in_=x_dram[:, ROUND:BATCH, :])
        plus_one = keep.tile([P, P], BF16)
        nc.vector.tensor_copy(out=plus_one[:], in_=ident[:])
        minus_one = keep.tile([P, P], BF16)
        nc.vector.tensor_scalar_mul(out=minus_one[:], in0=ident[:], scalar1=-1.0)

        def transpose_round(n):
            b, first = place(n)
            for j in range(ROUND):
                words = x_sb[b][:, first + j, :].bitcast(F32)
                xt = psum_t.tile([P, PASSES, 2, P], F32)
                for g in range(PASSES):
                    for u in range(2):
                        nc.tensor.transpose(
                            xt[:, g, u, :],
                            words[:, 2 * P * g + u : 2 * P * (g + 1) : 2],
                            ident[:],
                        )
                transposed[n, j] = xt

        def collect_round(n):
            grouped[n] = stage.tile([P, ROUND, PASSES, P, PACK], BF16, align_bytes=64, name="grouped")
            for j in range(ROUND):
                copy_out = nc.vector.tensor_copy if (n, j) == (0, 1) else nc.scalar.copy
                copy_out(
                    out=grouped[n][:, j]
                    .rearrange("p g r t -> p (g r t)")
                    .bitcast(F32)
                    .rearrange("p (g r u) -> p g r u", g=PASSES, u=2),
                    in_=transposed[n, j][:].rearrange("p g u r -> p g r u"),
                )

        def quantise_round(n):
            codes[n] = keep.tile([P, ROUND, PASSES, P], U32, align_bytes=64, name="codes%d" % n)
            planes[n] = keep.tile([P, ROUND, PASSES, P], U8, align_bytes=64, name="planes%d" % n)
            for j in range(ROUND):
                nc.vector.quantize_mx(
                    out=codes[n][:, j].rearrange("p g r -> p (g r)").bitcast(FP8X4),
                    scales=planes[n][:, j].rearrange("p g r -> p (g r)"),
                    in_=grouped[n][:, j].rearrange("p g r t -> p (g r t)"),
                )

        def project_round(n):
            for j in range(ROUND):
                acc = psum_o.tile([P, FEATURES], F32)
                for g in range(PASSES):
                    nc.tensor.matmul_mx(
                        out=acc[:],
                        lhsT=codes[n][:, j, g, :].bitcast(FP8X4),
                        lhsT_scale=planes[n][:, j, g, :],
                        rhs=w_codes[:, g, :].bitcast(FP8X4),
                        rhs_scale=w_planes[:, g, :],
                        start=(g == 0),
                        stop=(g == PASSES - 1),
                    )
                products[n, j] = acc

        def square_round(n, tiles):
            if tiles.start == 0:
                square_sums[n] = small.tile([P, ROUND, HEADS], F32, name="square_sum")
            for j in range(tiles.start, tiles.stop):
                for h in range(HEADS):
                    squares = stage.tile([P, D], BF16)
                    nc.scalar.activation(
                        out=squares[:],
                        in_=products[n, j][:, D * h : D * (h + 1)],
                        func=ACT.Square,
                        accum_out=square_sums[n][:, j, h : h + 1],
                    )

        def inverse_rms_round(n, tiles):
            if tiles.start == 0:
                rstd[n] = small.tile([P, ROUND, HEADS], F32, name="inv_rms")
            nc.scalar.activation(
                out=rstd[n][:, tiles, :].rearrange("p j h -> p (j h)"),
                in_=square_sums[n][:, tiles, :].rearrange("p j h -> p (j h)"),
                func=ACT.Abs_reciprocal_sqrt,
                bias=eps[:],
                scale=1.0 / D,
            )

        def tables_round(n):
            b, first = place(n)
            tiles = slice(first, first + ROUND)
            tables[n] = psum_c.tile([P, 2, ROUND, D], F32, name="tables")
            nc.tensor.matmul(
                out=tables[n][:, 0], lhsT=plus_one[:], rhs=cos_sb[b][:, tiles, :], start=True, stop=True
            )
            nc.tensor.matmul(
                out=tables[n][:, 1, :, low], lhsT=minus_one[:], rhs=sin_sb[b][:, tiles, low], start=True, stop=True
            )
            nc.tensor.matmul(
                out=tables[n][:, 1, :, high], lhsT=plus_one[:], rhs=sin_sb[b][:, tiles, high], start=True, stop=True
            )

        def normalise_round(n):
            b, first = place(n)
            normed[n] = keep.tile([P, ROPE_HEADS, ROUND, D], F32, name="normed%d" % n)
            for j in range(ROUND):
                acc = products[n, j]
                for h in range(ROPE_HEADS):
                    nc.vector.scalar_tensor_tensor(
                        out=normed[n][:, h, j, :],
                        in0=acc[:, D * h : D * (h + 1)],
                        scalar=rstd[n][:, j, h : h + 1],
                        in1=gain_of_head[h][:],
                        op0=ALU.mult,
                        op1=ALU.mult,
                    )
                if n < ROUNDS - SCALAR_VALUE_ROUNDS:
                    nc.vector.tensor_scalar_mul(
                        out=value[b][:, first + j, :],
                        in0=acc[:, D * ROPE_HEADS : FEATURES],
                        scalar1=rstd[n][:, j, ROPE_HEADS:HEADS],
                    )

        def scalar_value_round(n):
            b, first = place(n)
            for j in range(ROUND):
                nc.scalar.activation(
                    out=value[b][:, first + j, :],
                    in_=products[n, j][:, D * ROPE_HEADS : FEATURES],
                    func=ACT.Copy,
                    scale=rstd[n][:, j, ROPE_HEADS:HEADS],
                )

        def key_times_cos_round(n):
            b, first = place(n)
            nc.gpsimd.tensor_tensor(
                out=rope_products[n][:, 0, QUERY_HEADS],
                in0=normed[n][:, QUERY_HEADS],
                in1=cos_sb[b][:, first : first + ROUND, :],
                op=ALU.mult,
            )

        def store_values(b, tiles):
            dram_tiles = slice(BATCH * b + tiles.start, BATCH * b + tiles.stop)
            nc.sync.dma_start(out=v_dram[:, 0, dram_tiles, :], in_=value[b][:, tiles, :])

        def store_queries(b, tiles):
            dram_tiles = slice(BATCH * b + tiles.start, BATCH * b + tiles.stop)
            nc.sync.dma_start(out=q_dram[:, :, dram_tiles, :], in_=rotated[b][:, QUERIES, tiles, :])

        def store_key(b, tiles):
            dram_tiles = slice(BATCH * b + tiles.start, BATCH * b + tiles.stop)
            nc.sync.dma_start(out=k_dram[:, 0, dram_tiles, :], in_=rotated[b][:, QUERY_HEADS, tiles, :])

        def store_all(b, tiles):
            store_values(b, tiles)
            store_queries(b, tiles)
            store_key(b, tiles)

        def multiply_round(n):
            both = rope_products[n]
            heads = ROPE_HEADS if n == LAST else QUERY_HEADS
            nc.vector.tensor_tensor(
                out=both[:, 0, 0:heads],
                in0=normed[n][:, 0:heads],
                in1=tables[n][:, 0].unsqueeze(1).to_broadcast([P, heads, ROUND, D]),
                op=ALU.mult,
            )
            nc.vector.tensor_tensor(
                out=both[:, 1].rearrange("p h j (w d) -> p h j w d", w=2),
                in0=normed[n][:].rearrange("p h j (w d) -> p h j w d", w=2)[:, :, :, ::-1, :],
                in1=tables[n][:, 1]
                .rearrange("p j (w d) -> p j w d", w=2)
                .unsqueeze(1)
                .to_broadcast([P, ROPE_HEADS, ROUND, 2, HALF]),
                op=ALU.mult,
            )

        def join_round(engine, n, heads):
            b, first = place(n)
            engine.tensor_tensor(
                out=rotated[b][:, heads, first : first + ROUND, :],
                in0=rope_products[n][:, 0, heads],
                in1=rope_products[n][:, 1, heads],
                op=ALU.add,
            )

        def finish_round(n):
            b, first = place(n)
            tiles = slice(first, first + ROUND)
            if n < LAST:
                join_round(nc.gpsimd, n, ALL_ROPE)
                if n == LAST - 1:
                    store_all(b, tiles)
                elif tiles.stop == BATCH:
                    store_all(b, slice(0, BATCH))
            else:
                store_values(b, tiles)
                join_round(nc.vector, n, QUERIES)
                store_queries(b, tiles)
                join_round(nc.vector, n, KEY)
                store_key(b, tiles)

        transpose_round(0)
        collect_round(0)
        quantise_round(0)
        transpose_round(1)
        project_round(0)
        collect_round(1)
        square_round(0, both_tiles)
        inverse_rms_round(0, both_tiles)
        tables_round(0)
        transpose_round(2)
        quantise_round(1)
        project_round(1)
        collect_round(2)
        transpose_round(3)
        for n in range(ROUNDS):
            b, first = place(n)
            if first == 0:
                if b + X_BATCHES_AHEAD < BATCHES:
                    load_x(b + X_BATCHES_AHEAD)
                if b + TABLE_BATCHES_AHEAD < BATCHES:
                    load_tables(b + TABLE_BATCHES_AHEAD)
                rotated[b] = results.tile([P, ROPE_HEADS, BATCH, D], F32, name="rotated")
            normalise_round(n)
            rope_products[n] = stage.tile([P, 2, ROPE_HEADS, ROUND, D], F32, name="rope_products")
            if n < LAST:
                key_times_cos_round(n)
            if n + SQUARE_LEAD <= LAST:
                for tiles in single_tiles if n + SQUARE_LEAD == LAST else (both_tiles,):
                    square_round(n + SQUARE_LEAD, tiles)
                    inverse_rms_round(n + SQUARE_LEAD, tiles)
            if n + COLLECT_LEAD <= LAST:
                collect_round(n + COLLECT_LEAD)
            if n + TABLES_LEAD <= LAST:
                tables_round(n + TABLES_LEAD)
            if n >= ROUNDS - SCALAR_VALUE_ROUNDS:
                scalar_value_round(n)
            multiply_round(n)
            finish_round(n)
            if n + QUANTISE_LEAD <= LAST:
                quantise_round(n + QUANTISE_LEAD)
            if n + PROJECT_LEAD <= LAST:
                project_round(n + PROJECT_LEAD)
            if n + TRANSPOSE_LEAD <= LAST:
                transpose_round(n + TRANSPOSE_LEAD)
